import numpy as np
import ml_dtypes


def mxq(x, axis, fmt="e4m3"):
    dtype, down = {"e4m3": (ml_dtypes.float8_e4m3fn, 7), "e5m2": (ml_dtypes.float8_e5m2, 14)}[fmt]
    v = np.moveaxis(np.asarray(x, np.float32).astype(ml_dtypes.bfloat16).astype(np.float64), axis, -1)
    blocks = v.reshape(v.shape[:-1] + (-1, 32))
    amax = np.abs(blocks).max(-1, keepdims=True)
    byte = np.maximum(np.where(amax > 0, np.frexp(amax)[1] - 1 + 127, 0) - down, 1)
    scale = np.exp2(byte - 127.0)
    codes = (blocks / scale).astype(np.float32).astype(dtype).astype(np.float64)
    return np.moveaxis((codes * scale).reshape(v.shape), -1, axis)


BF16 = ml_dtypes.bfloat16


def bf(x):
    return np.asarray(x, np.float32).astype(BF16)


def f64(x):
    return np.asarray(x).astype(np.float64)


N, B, T, C, R, O, NC, H, W = 4, 4096, 4, 256, 4, 512, 256, 16, 4
BN_EPS = 1e-5
L2_EPS = 1e-12


def setup_inputs():
    off = 1.5 * np.random.standard_normal((N, 1, O))
    sd = 0.3 + 0.6 * np.random.random_sample((N, 1, O))
    col = (0.5 + np.random.random_sample((N, 1, NC))) / np.sqrt(O)
    return {"emb": bf(off + sd * np.random.standard_normal((N, B, O))),
            "gamma": bf(1.0 + 0.1 * np.random.standard_normal((N, O))),
            "beta": bf(0.1 * np.random.standard_normal((N, O))),
            "fc1d": bf(col * np.random.standard_normal((N, O, NC)))}


def reference(emb, gamma, beta, fc1d):
    e = f64(emb)
    mean = e.mean(axis=1, keepdims=True)
    var = ((e - mean) ** 2).mean(axis=1, keepdims=True)
    bn = f64(gamma)[:, None, :] * (e - mean) / np.sqrt(var + BN_EPS) + f64(beta)[:, None, :]
    bnn = bn / np.maximum(np.sqrt((bn ** 2).sum(axis=-1, keepdims=True)), L2_EPS)
    fc = f64(fc1d)
    fcn = fc / np.maximum(np.sqrt((fc ** 2).sum(axis=1, keepdims=True)), L2_EPS)
    logits = mxq(bnn, 2, "e4m3") @ mxq(fcn, 1, "e4m3")
    return np.transpose(logits, (1, 0, 2))

@@ -1,0 +1,230 @@
+from contextlib import ExitStack
+
+import concourse.mybir as mybir
+from concourse.masks import make_identity
+
+F32 = mybir.dt.float32
+BF16 = mybir.dt.bfloat16
+U32 = mybir.dt.uint32
+U8 = mybir.dt.uint8
+FP8X4 = mybir.dt.float8_e4m3fn_x4
+ALU = mybir.AluOpType
+ACT = mybir.ActivationFunctionType
+
+BINS = 4
+SAMPLES = 4096
+FEATURES = 512
+CLASSES = 256
+BN_EPS = 1e-5
+L2_EPS = 1e-12
+
+P = 128
+PACK = 4
+HALVES = 2
+PAIR = 2
+TILES = SAMPLES // P
+GROUP = 4
+GROUPS = TILES // GROUP
+COLS = GROUP * P
+CLASS_TILES = CLASSES // P
+BN_CHUNK = 512
+CHUNKS = COLS * PAIR // BN_CHUNK
+BANK_TILES = 2
+STATS = 6
+
+FLOPS = 2 * BINS * SAMPLES * FEATURES * CLASSES
+
+AFFINE_LAG = GROUPS
+NORM_LAG = AFFINE_LAG + 1
+SCALE_LAG = NORM_LAG + 1
+MATMUL_LAG = SCALE_LAG + 1
+
+
+def tile_gmpahead_pb_t_kernel(tc, emb, gamma, beta, fc1d, out):
+    nc = tc.nc
+    emb_tiles = emb.rearrange("n (p j) o -> n p j o", j=TILES)
+    out_tiles = out.rearrange("(p j) n k -> p j n k", j=TILES)
+    all_groups = BINS * GROUPS
+
+    with ExitStack() as stack:
+        const = stack.enter_context(tc.tile_pool(name="const", bufs=1))
+        loads = stack.enter_context(tc.tile_pool(name="loads", bufs=6))
+        turned = stack.enter_context(tc.tile_pool(name="turned", bufs=AFFINE_LAG + 2))
+        columns = stack.enter_context(tc.tile_pool(name="columns", bufs=4))
+        classifier = stack.enter_context(tc.tile_pool(name="classifier", bufs=2))
+        small = stack.enter_context(tc.tile_pool(name="small", bufs=4))
+        per_bin = stack.enter_context(tc.tile_pool(name="per_bin", bufs=2))
+        scrap = stack.enter_context(tc.tile_pool(name="scrap", bufs=4))
+        quant = stack.enter_context(tc.tile_pool(name="quant", bufs=3))
+        results = stack.enter_context(tc.tile_pool(name="results", bufs=4))
+        psum_raw = stack.enter_context(tc.psum_pool(name="psum_raw", bufs=2))
+        psum_back = stack.enter_context(tc.psum_pool(name="psum_back", bufs=3))
+        psum_spread = stack.enter_context(tc.psum_pool(name="psum_spread", bufs=1))
+        psum_out = stack.enter_context(tc.psum_pool(name="psum_out", bufs=2))
+
+        ident = const.tile([P, P], F32)
+        make_identity(nc, ident[:])
+
+        gb_rows = const.tile([P, HALVES * P], F32)
+        nc.vector.memset(gb_rows[:], 0.0)
+        nc.scalar.dma_start(out=gb_rows[0:BINS, :].bitcast(BF16), in_=gamma)
+        nc.scalar.dma_start(out=gb_rows[BINS : 2 * BINS, :].bitcast(BF16), in_=beta)
+        bank = psum_raw.tile([P, COLS], F32)
+        for u in range(HALVES):
+            nc.tensor.transpose(out=bank[:, u * P : (u + 1) * P], in_=gb_rows[:, u * P : (u + 1) * P], identity=ident[:])
+        gb_t = const.tile([P, 2 * BINS, PACK], F32)
+        nc.vector.tensor_copy(
+            out=gb_t[:].rearrange("p r (u e) -> p r u e", e=PAIR),
+            in_=bank[:, 0 : HALVES * P].bitcast(BF16).rearrange("p (u r e) -> p r u e", u=HALVES, e=PAIR)[:, 0 : 2 * BINS, :, :],
+        )
+
+        fc_raw = const.tile([P, BINS * HALVES, PAIR * CLASSES], BF16)
+        nc.scalar.dma_start(out=fc_raw[:], in_=fc1d.rearrange("n (u p e) k -> p (n u) (e k)", u=HALVES, e=PAIR))
+        fc_codes = const.tile([P, BINS, CLASSES], U32, align_bytes=64)
+        fc_planes = const.tile([P, BINS, CLASSES], U8, align_bytes=64)
+
+        def inverse_column_norms(x_t, n_tiles):
+            norm_sq = small.tile([P, GROUP], F32)
+            for j in range(n_tiles):
+                back = psum_back.tile([P, PACK * P], F32)
+                for t in range(PACK):
+                    nc.tensor.transpose(out=back[:, t * P : (t + 1) * P], in_=x_t[:, t, j * P : (j + 1) * P], identity=ident[:])
+                squares = scrap.tile([P, PACK * P], BF16)
+                nc.scalar.activation(out=squares[:], in_=back[:], func=ACT.Square, accum_out=norm_sq[:, j : j + 1])
+            clamped = small.tile([P, GROUP], F32)
+            nc.vector.tensor_scalar_max(out=clamped[:, 0:n_tiles], in0=norm_sq[:, 0:n_tiles], scalar1=L2_EPS * L2_EPS)
+            norm = small.tile([P, GROUP], F32)
+            nc.scalar.sqrt(out=norm[:, 0:n_tiles], in_=clamped[:, 0:n_tiles])
+            inverse = small.tile([P, GROUP], F32)
+            nc.vector.reciprocal(out=inverse[:, 0:n_tiles], in_=norm[:, 0:n_tiles])
+            return inverse
+
+        def scale_columns_and_quantise(x_t, inverse, n_tiles, codes, plane):
+            cols = n_tiles * P
+            spread = psum_spread.tile([P, COLS], F32)
+            for j in range(n_tiles):
+                nc.tensor.transpose(out=spread[:, j * P : (j + 1) * P], in_=inverse[:, j : j + 1].to_broadcast([P, P]), identity=ident[:])
+            grouped = quant.tile([P, COLS, PACK], BF16, align_bytes=64)
+            nc.vector.tensor_tensor(
+                out=grouped[:, 0:cols, :],
+                in0=x_t.rearrange("p t c -> p c t"),
+                in1=spread[:, 0:cols].unsqueeze(2).to_broadcast([P, cols, PACK]),
+                op=ALU.mult,
+            )
+            nc.vector.quantize_mx(out=codes.bitcast(FP8X4), scales=plane, in_=grouped[:, 0:cols, :].rearrange("p c t -> p (c t)"))
+
+        stats_of = {}
+        coefficients_of = {}
+        turned_of = {}
+        columns_of = {}
+        inverse_of = {}
+        operand_of = {}
+        fc_columns_of = {}
+        fc_inverse_of = {}
+
+        def statistics_stage(group):
+            n, g = divmod(group, GROUPS)
+            raw = loads.tile([P, GROUP * FEATURES], BF16)
+            nc.sync.dma_start(out=raw[:].rearrange("p (j o) -> p j o", j=GROUP), in_=emb_tiles[n, :, g * GROUP : (g + 1) * GROUP, :])
+            words = raw[:].bitcast(F32)
+            if g == 0:
+                stats = per_bin.tile([P, HALVES, GROUPS * CHUNKS, STATS], F32)
+                stats_of[n] = stats
+            e_t = turned.tile([P, HALVES * COLS], F32)
+            turned_of[group] = e_t
+            for u in range(HALVES):
+                bank = psum_raw.tile([P, COLS], F32)
+                for j in range(GROUP):
+                    first = (j * HALVES + u) * P
+                    nc.tensor.transpose(out=bank[:, j * P : (j + 1) * P], in_=words[:, first : first + P], identity=ident[:])
+                nc.scalar.copy(out=e_t[:, u * COLS : (u + 1) * COLS], in_=bank[:])
+                values = e_t[:, u * COLS : (u + 1) * COLS].bitcast(BF16)
+                for h in range(CHUNKS):
+                    nc.vector.bn_stats(out=stats_of[n][:, u, g * CHUNKS + h, :], in_=values[:, h * BN_CHUNK : (h + 1) * BN_CHUNK])
+
+        def coefficients(n):
+            moments = per_bin.tile([P, PACK, 2], F32)
+            for u in range(HALVES):
+                for e in range(PAIR):
+                    nc.vector.bn_aggr(out=moments[:, PAIR * u + e, :], in_=stats_of[n][:, u, :, 3 * e : 3 * e + 3])
+            var_eps = per_bin.tile([P, PACK], F32)
+            nc.vector.tensor_scalar_add(out=var_eps[:], in0=moments[:, :, 1], scalar1=BN_EPS)
+            std = per_bin.tile([P, PACK], F32)
+            nc.scalar.sqrt(out=std[:], in_=var_eps[:])
+            rstd = per_bin.tile([P, PACK], F32)
+            nc.vector.reciprocal(out=rstd[:], in_=std[:])
+            gain = per_bin.tile([P, PACK], F32)
+            nc.vector.tensor_mul(out=gain[:], in0=gb_t[:, n, :], in1=rstd[:])
+            gain_mean = per_bin.tile([P, PACK], F32)
+            nc.vector.tensor_mul(out=gain_mean[:], in0=gain[:], in1=moments[:, :, 0])
+            shift = per_bin.tile([P, PACK], F32)
+            nc.vector.tensor_sub(out=shift[:], in0=gb_t[:, BINS + n, :], in1=gain_mean[:])
+            coefficients_of[n] = (gain, shift)
+
+        def affine_stage(group):
+            gain, shift = coefficients_of[group // GROUPS]
+            y_t = columns.tile([P, PACK, COLS], F32)
+            columns_of[group] = y_t
+            for u in range(HALVES):
+                values = turned_of[group][:, u * COLS : (u + 1) * COLS].bitcast(BF16).rearrange("p (c e) -> p c e", e=PAIR)
+                for e in range(PAIR):
+                    t = PAIR * u + e
+                    nc.gpsimd.tensor_scalar(
+                        out=y_t[:, t, :], in0=values[:, :, e], scalar1=gain[:, t : t + 1], scalar2=shift[:, t : t + 1], op0=ALU.mult, op1=ALU.add
+                    )
+
+        def norm_stage(group):
+            inverse_of[group] = inverse_column_norms(columns_of[group], GROUP)
+
+        def scale_stage(group):
+            codes = quant.tile([P, COLS], U32, align_bytes=64)
+            plane = quant.tile([P, COLS], U8, align_bytes=64)
+            operand_of[group] = (codes, plane)
+            scale_columns_and_quantise(columns_of[group], inverse_of[group], GROUP, codes[:], plane[:])
+
+        def matmul_stage(group):
+            n, g = divmod(group, GROUPS)
+            codes, plane = operand_of[group]
+            logits = results.tile([P, GROUP, CLASSES], F32)
+            for first in range(0, GROUP, BANK_TILES):
+                acc = psum_out.tile([P, BANK_TILES, CLASSES], F32)
+                for i in range(BANK_TILES):
+                    samples = slice((first + i) * P, (first + i + 1) * P)
+                    nc.tensor.matmul_mx(
+                        out=acc[:, i, :],
+                        lhsT=codes[:, samples].bitcast(FP8X4),
+                        lhsT_scale=plane[:, samples],
+                        rhs=fc_codes[:, n, :].bitcast(FP8X4),
+                        rhs_scale=fc_planes[:, n, :],
+                        start=True,
+                        stop=True,
+                    )
+                nc.scalar.copy(out=logits[:, first : first + BANK_TILES, :], in_=acc[:])
+            nc.scalar.dma_start(out=out_tiles[:, g * GROUP : (g + 1) * GROUP, n, :], in_=logits[:])
+
+        def classifier_norm_stage(n):
+            fc_t = classifier.tile([P, PACK, CLASSES], F32)
+            fc_columns_of[n] = fc_t
+            nc.scalar.copy(out=fc_t[:], in_=fc_raw[:, n * HALVES : (n + 1) * HALVES, :].rearrange("p u (e k) -> p (u e) k", e=PAIR))
+            fc_inverse_of[n] = inverse_column_norms(fc_t, CLASS_TILES)
+
+        def classifier_scale_stage(n):
+            scale_columns_and_quantise(fc_columns_of[n], fc_inverse_of[n], CLASS_TILES, fc_codes[:, n, :], fc_planes[:, n, :])
+
+        for step in range(all_groups + MATMUL_LAG):
+            if 0 <= step - MATMUL_LAG:
+                matmul_stage(step - MATMUL_LAG)
+            if 0 <= step - SCALE_LAG < all_groups:
+                scale_stage(step - SCALE_LAG)
+            if 0 <= step - NORM_LAG < all_groups:
+                norm_stage(step - NORM_LAG)
+            if 0 <= step - AFFINE_LAG < all_groups:
+                affine_stage(step - AFFINE_LAG)
+            if step < 2 * BINS and step % 2 == 1:
+                classifier_scale_stage(step // 2)
+            if step < 2 * BINS and step % 2 == 0:
+                classifier_norm_stage(step // 2)
+            if step < all_groups:
+                statistics_stage(step)
+                if step % GROUPS == GROUPS - 1:
+                    coefficients(step // GROUPS)

@@ -25,6 +25,7 @@ PAIR = 2
 TILES = SAMPLES // P
 GROUP = 4
 GROUPS = TILES // GROUP
+ALL_GROUPS = BINS * GROUPS
 COLS = GROUP * P
 CLASS_TILES = CLASSES // P
 BN_CHUNK = 512
@@ -34,33 +35,43 @@ STATS = 6
 
 FLOPS = 2 * BINS * SAMPLES * FEATURES * CLASSES
 
-AFFINE_LAG = GROUPS
-NORM_LAG = AFFINE_LAG + 1
-SCALE_LAG = NORM_LAG + 1
-MATMUL_LAG = SCALE_LAG + 1
+LOAD_LEAD = 3
+STATS_LAG = 1
+MOMENTS_LAG = GROUPS - 1 + STATS_LAG
+DEVIATION_LAG = MOMENTS_LAG + 1
+COEFFICIENTS_LAG = DEVIATION_LAG + 1
+AFFINE_LAG = COEFFICIENTS_LAG + 1
+SQUARES_LAG = AFFINE_LAG + 1
+NORM_AFTER = 1
+INVERSE_AFTER = 2
+SCALE_AFTER = 3
+MATMUL_AFTER = 4
+SMALL_INPUTS_STEP = 2
+LAST_STEP = ALL_GROUPS - 1 + SQUARES_LAG + MATMUL_AFTER
+
+SCALAR_BANKS = 6
+SPREAD_BANKS = 2
 
 
 def tile_gmpahead_pb_t_kernel(tc, emb, gamma, beta, fc1d, out):
     nc = tc.nc
     emb_tiles = emb.rearrange("n (p j) o -> n p j o", j=TILES)
     out_tiles = out.rearrange("(p j) n k -> p j n k", j=TILES)
-    all_groups = BINS * GROUPS
 
     with ExitStack() as stack:
         const = stack.enter_context(tc.tile_pool(name="const", bufs=1))
-        loads = stack.enter_context(tc.tile_pool(name="loads", bufs=6))
+        loads = stack.enter_context(tc.tile_pool(name="loads", bufs=LOAD_LEAD + 2))
         turned = stack.enter_context(tc.tile_pool(name="turned", bufs=AFFINE_LAG + 2))
-        columns = stack.enter_context(tc.tile_pool(name="columns", bufs=4))
-        classifier = stack.enter_context(tc.tile_pool(name="classifier", bufs=2))
+        columns = stack.enter_context(tc.tile_pool(name="columns", bufs=SQUARES_LAG - AFFINE_LAG + SCALE_AFTER + 2))
+        classifier = stack.enter_context(tc.tile_pool(name="classifier", bufs=SCALE_AFTER + 1))
         small = stack.enter_context(tc.tile_pool(name="small", bufs=4))
         per_bin = stack.enter_context(tc.tile_pool(name="per_bin", bufs=2))
         scrap = stack.enter_context(tc.tile_pool(name="scrap", bufs=4))
         quant = stack.enter_context(tc.tile_pool(name="quant", bufs=3))
         results = stack.enter_context(tc.tile_pool(name="results", bufs=4))
-        psum_raw = stack.enter_context(tc.psum_pool(name="psum_raw", bufs=2))
-        psum_back = stack.enter_context(tc.psum_pool(name="psum_back", bufs=3))
-        psum_spread = stack.enter_context(tc.psum_pool(name="psum_spread", bufs=1))
-        psum_out = stack.enter_context(tc.psum_pool(name="psum_out", bufs=2))
+        psum_scalar = stack.enter_context(tc.psum_pool(name="psum_scalar", bufs=SCALAR_BANKS))
+        psum_spread = stack.enter_context(tc.psum_pool(name="psum_spread", bufs=SPREAD_BANKS))
+        stack.enter_context(tc.manual_schedule())
 
         ident = const.tile([P, P], F32)
         make_identity(nc, ident[:])
@@ -69,94 +80,98 @@ def tile_gmpahead_pb_t_kernel(tc, emb, gamma, beta, fc1d, out):
         nc.vector.memset(gb_rows[:], 0.0)
         nc.scalar.dma_start(out=gb_rows[0:BINS, :].bitcast(BF16), in_=gamma)
         nc.scalar.dma_start(out=gb_rows[BINS : 2 * BINS, :].bitcast(BF16), in_=beta)
-        bank = psum_raw.tile([P, COLS], F32)
-        for u in range(HALVES):
-            nc.tensor.transpose(out=bank[:, u * P : (u + 1) * P], in_=gb_rows[:, u * P : (u + 1) * P], identity=ident[:])
         gb_t = const.tile([P, 2 * BINS, PACK], F32)
-        nc.vector.tensor_copy(
-            out=gb_t[:].rearrange("p r (u e) -> p r u e", e=PAIR),
-            in_=bank[:, 0 : HALVES * P].bitcast(BF16).rearrange("p (u r e) -> p r u e", u=HALVES, e=PAIR)[:, 0 : 2 * BINS, :, :],
-        )
-
         fc_raw = const.tile([P, BINS * HALVES, PAIR * CLASSES], BF16)
         nc.scalar.dma_start(out=fc_raw[:], in_=fc1d.rearrange("n (u p e) k -> p (n u) (e k)", u=HALVES, e=PAIR))
         fc_codes = const.tile([P, BINS, CLASSES], U32, align_bytes=64)
         fc_planes = const.tile([P, BINS, CLASSES], U8, align_bytes=64)
 
-        def inverse_column_norms(x_t, n_tiles):
-            norm_sq = small.tile([P, GROUP], F32)
-            for j in range(n_tiles):
-                back = psum_back.tile([P, PACK * P], F32)
-                for t in range(PACK):
-                    nc.tensor.transpose(out=back[:, t * P : (t + 1) * P], in_=x_t[:, t, j * P : (j + 1) * P], identity=ident[:])
-                squares = scrap.tile([P, PACK * P], BF16)
-                nc.scalar.activation(out=squares[:], in_=back[:], func=ACT.Square, accum_out=norm_sq[:, j : j + 1])
-            clamped = small.tile([P, GROUP], F32)
-            nc.vector.tensor_scalar_max(out=clamped[:, 0:n_tiles], in0=norm_sq[:, 0:n_tiles], scalar1=L2_EPS * L2_EPS)
-            norm = small.tile([P, GROUP], F32)
-            nc.scalar.sqrt(out=norm[:, 0:n_tiles], in_=clamped[:, 0:n_tiles])
-            inverse = small.tile([P, GROUP], F32)
-            nc.vector.reciprocal(out=inverse[:, 0:n_tiles], in_=norm[:, 0:n_tiles])
-            return inverse
-
-        def scale_columns_and_quantise(x_t, inverse, n_tiles, codes, plane):
-            cols = n_tiles * P
-            spread = psum_spread.tile([P, COLS], F32)
-            for j in range(n_tiles):
-                nc.tensor.transpose(out=spread[:, j * P : (j + 1) * P], in_=inverse[:, j : j + 1].to_broadcast([P, P]), identity=ident[:])
-            grouped = quant.tile([P, COLS, PACK], BF16, align_bytes=64)
-            nc.vector.tensor_tensor(
-                out=grouped[:, 0:cols, :],
-                in0=x_t.rearrange("p t c -> p c t"),
-                in1=spread[:, 0:cols].unsqueeze(2).to_broadcast([P, cols, PACK]),
-                op=ALU.mult,
-            )
-            nc.vector.quantize_mx(out=codes.bitcast(FP8X4), scales=plane, in_=grouped[:, 0:cols, :].rearrange("p c t -> p (c t)"))
-
-        stats_of = {}
-        coefficients_of = {}
+        loaded_of = {}
         turned_of = {}
+        stats_of = {}
+        moments_of = {}
+        deviation_of = {}
+        coefficients_of = {}
+        product_of = {}
+        gb_bank = {}
         columns_of = {}
+        norm_sq_of = {}
+        clamped_of = {}
+        norm_of = {}
         inverse_of = {}
+        spread_of = {}
+        grouped_of = {}
         operand_of = {}
-        fc_columns_of = {}
-        fc_inverse_of = {}
 
-        def statistics_stage(group):
+        def is_group(group):
+            return 0 <= group < ALL_GROUPS
+
+        def is_bin(n):
+            return 0 <= n < BINS
+
+        def bin_due(step, lag):
+            n, rest = divmod(step - lag, GROUPS)
+            return [n] if rest == 0 and is_bin(n) else []
+
+        def columns_due(step):
+            keys = []
+            if is_group(step - SQUARES_LAG):
+                keys.append(("samples", step - SQUARES_LAG))
+            if is_bin(step - SMALL_INPUTS_STEP):
+                keys.append(("classes", step - SMALL_INPUTS_STEP))
+            return keys
+
+        def tiles_of(key):
+            return GROUP if key[0] == "samples" else CLASS_TILES
+
+
+        def load_stage(group):
             n, g = divmod(group, GROUPS)
             raw = loads.tile([P, GROUP * FEATURES], BF16)
+            loaded_of[group] = raw
             nc.sync.dma_start(out=raw[:].rearrange("p (j o) -> p j o", j=GROUP), in_=emb_tiles[n, :, g * GROUP : (g + 1) * GROUP, :])
-            words = raw[:].bitcast(F32)
-            if g == 0:
-                stats = per_bin.tile([P, HALVES, GROUPS * CHUNKS, STATS], F32)
-                stats_of[n] = stats
+
+        def turn_stage(group):
+            words = loaded_of[group][:].bitcast(F32)
             e_t = turned.tile([P, HALVES * COLS], F32)
             turned_of[group] = e_t
             for u in range(HALVES):
-                bank = psum_raw.tile([P, COLS], F32)
+                bank = psum_scalar.tile([P, COLS], F32, tag="bank")
                 for j in range(GROUP):
                     first = (j * HALVES + u) * P
                     nc.tensor.transpose(out=bank[:, j * P : (j + 1) * P], in_=words[:, first : first + P], identity=ident[:])
                 nc.scalar.copy(out=e_t[:, u * COLS : (u + 1) * COLS], in_=bank[:])
-                values = e_t[:, u * COLS : (u + 1) * COLS].bitcast(BF16)
-                for h in range(CHUNKS):
-                    nc.vector.bn_stats(out=stats_of[n][:, u, g * CHUNKS + h, :], in_=values[:, h * BN_CHUNK : (h + 1) * BN_CHUNK])
 
-        def coefficients(n):
+        def statistics_stage(group, u):
+            n, g = divmod(group, GROUPS)
+            if g == 0 and u == 0:
+                stats = per_bin.tile([P, HALVES, GROUPS * CHUNKS, STATS], F32)
+                stats_of[n] = stats
+            values = turned_of[group][:, u * COLS : (u + 1) * COLS].bitcast(BF16)
+            for h in range(CHUNKS):
+                nc.vector.bn_stats(out=stats_of[n][:, u, g * CHUNKS + h, :], in_=values[:, h * BN_CHUNK : (h + 1) * BN_CHUNK])
+
+        def moments_stage(n):
             moments = per_bin.tile([P, PACK, 2], F32)
             for u in range(HALVES):
                 for e in range(PAIR):
                     nc.vector.bn_aggr(out=moments[:, PAIR * u + e, :], in_=stats_of[n][:, u, :, 3 * e : 3 * e + 3])
             var_eps = per_bin.tile([P, PACK], F32)
             nc.vector.tensor_scalar_add(out=var_eps[:], in0=moments[:, :, 1], scalar1=BN_EPS)
+            moments_of[n] = (moments, var_eps)
+
+        def deviation_stage(n):
             std = per_bin.tile([P, PACK], F32)
-            nc.scalar.sqrt(out=std[:], in_=var_eps[:])
+            deviation_of[n] = std
+            nc.scalar.sqrt(out=std[:], in_=moments_of[n][1][:])
+
+        def coefficients_stage(n):
             rstd = per_bin.tile([P, PACK], F32)
-            nc.vector.reciprocal(out=rstd[:], in_=std[:])
+            nc.vector.reciprocal(out=rstd[:], in_=deviation_of[n][:])
             gain = per_bin.tile([P, PACK], F32)
             nc.vector.tensor_mul(out=gain[:], in0=gb_t[:, n, :], in1=rstd[:])
             gain_mean = per_bin.tile([P, PACK], F32)
-            nc.vector.tensor_mul(out=gain_mean[:], in0=gain[:], in1=moments[:, :, 0])
+            nc.vector.tensor_mul(out=gain_mean[:], in0=gain[:], in1=moments_of[n][0][:, :, 0])
             shift = per_bin.tile([P, PACK], F32)
             nc.vector.tensor_sub(out=shift[:], in0=gb_t[:, BINS + n, :], in1=gain_mean[:])
             coefficients_of[n] = (gain, shift)
@@ -164,7 +179,7 @@ def tile_gmpahead_pb_t_kernel(tc, emb, gamma, beta, fc1d, out):
         def affine_stage(group):
             gain, shift = coefficients_of[group // GROUPS]
             y_t = columns.tile([P, PACK, COLS], F32)
-            columns_of[group] = y_t
+            columns_of[("samples", group)] = y_t
             for u in range(HALVES):
                 values = turned_of[group][:, u * COLS : (u + 1) * COLS].bitcast(BF16).rearrange("p (c e) -> p c e", e=PAIR)
                 for e in range(PAIR):
@@ -173,58 +188,152 @@ def tile_gmpahead_pb_t_kernel(tc, emb, gamma, beta, fc1d, out):
                         out=y_t[:, t, :], in0=values[:, :, e], scalar1=gain[:, t : t + 1], scalar2=shift[:, t : t + 1], op0=ALU.mult, op1=ALU.add
                     )
 
-        def norm_stage(group):
-            inverse_of[group] = inverse_column_norms(columns_of[group], GROUP)
+        def classifier_cast(n):
+            fc_t = classifier.tile([P, PACK, CLASSES], F32)
+            columns_of[("classes", n)] = fc_t
+            nc.scalar.copy(out=fc_t[:], in_=fc_raw[:, n * HALVES : (n + 1) * HALVES, :].rearrange("p u (e k) -> p (u e) k", e=PAIR))
 
-        def scale_stage(group):
-            codes = quant.tile([P, COLS], U32, align_bytes=64)
-            plane = quant.tile([P, COLS], U8, align_bytes=64)
-            operand_of[group] = (codes, plane)
-            scale_columns_and_quantise(columns_of[group], inverse_of[group], GROUP, codes[:], plane[:])
+        def turn_gamma_and_beta():
+            spread = psum_spread.tile([P, COLS], F32)
+            gb_bank[0] = spread
+            for u in range(HALVES):
+                nc.tensor.transpose(out=spread[:, u * P : (u + 1) * P], in_=gb_rows[:, u * P : (u + 1) * P], identity=ident[:])
+
+        def keep_gamma_and_beta():
+            nc.vector.tensor_copy(
+                out=gb_t[:].rearrange("p r (u e) -> p r u e", e=PAIR),
+                in_=gb_bank[0][:, 0 : HALVES * P].bitcast(BF16).rearrange("p (u r e) -> p r u e", u=HALVES, e=PAIR)[:, 0 : 2 * BINS, :, :],
+            )
+
+
+        def squares_stage(key):
+            x_t = columns_of[key]
+            norm_sq = small.tile([P, GROUP], F32)
+            norm_sq_of[key] = norm_sq
+            for j in range(tiles_of(key)):
+                back = psum_scalar.tile([P, PACK * P], F32, tag="bank")
+                for t in range(PACK):
+                    nc.tensor.transpose(out=back[:, t * P : (t + 1) * P], in_=x_t[:, t, j * P : (j + 1) * P], identity=ident[:])
+                squares = scrap.tile([P, PACK * P], BF16)
+                nc.scalar.activation(out=squares[:], in_=back[:], func=ACT.Square, accum_out=norm_sq[:, j : j + 1])
+
+        def clamp_stage(key):
+            tiles = tiles_of(key)
+            clamped = small.tile([P, GROUP], F32)
+            clamped_of[key] = clamped
+            nc.vector.tensor_scalar_max(out=clamped[:, 0:tiles], in0=norm_sq_of[key][:, 0:tiles], scalar1=L2_EPS * L2_EPS)
+
+        def norm_stage(key):
+            tiles = tiles_of(key)
+            norm = small.tile([P, GROUP], F32)
+            norm_of[key] = norm
+            nc.scalar.sqrt(out=norm[:, 0:tiles], in_=clamped_of[key][:, 0:tiles])
+
+        def inverse_stage(key):
+            tiles = tiles_of(key)
+            inverse = small.tile([P, GROUP], F32)
+            inverse_of[key] = inverse
+            nc.vector.reciprocal(out=inverse[:, 0:tiles], in_=norm_of[key][:, 0:tiles])
+
+        def spread_stage(key):
+            spread = psum_spread.tile([P, COLS], F32)
+            spread_of[key] = spread
+            for j in range(tiles_of(key)):
+                nc.tensor.transpose(out=spread[:, j * P : (j + 1) * P], in_=inverse_of[key][:, j : j + 1].to_broadcast([P, P]), identity=ident[:])
+
+        def scale_stage(key):
+            cols = tiles_of(key) * P
+            grouped = quant.tile([P, COLS, PACK], BF16, align_bytes=64)
+            grouped_of[key] = grouped
+            nc.vector.tensor_tensor(
+                out=grouped[:, 0:cols, :],
+                in0=columns_of[key].rearrange("p t c -> p c t"),
+                in1=spread_of[key][:, 0:cols].unsqueeze(2).to_broadcast([P, cols, PACK]),
+                op=ALU.mult,
+            )
+
+        def quantise_stage(key):
+            cols = tiles_of(key) * P
+            if key[0] == "samples":
+                codes = quant.tile([P, COLS], U32, align_bytes=64)
+                plane = quant.tile([P, COLS], U8, align_bytes=64)
+                operand_of[key] = (codes[:], plane[:])
+            else:
+                operand_of[key] = (fc_codes[:, key[1], :], fc_planes[:, key[1], :])
+            nc.vector.quantize_mx(
+                out=operand_of[key][0].bitcast(FP8X4), scales=operand_of[key][1], in_=grouped_of[key][:, 0:cols, :].rearrange("p c t -> p (c t)")
+            )
+
 
         def matmul_stage(group):
-            n, g = divmod(group, GROUPS)
-            codes, plane = operand_of[group]
-            logits = results.tile([P, GROUP, CLASSES], F32)
+            codes, plane = operand_of[("samples", group)]
+            class_codes, class_plane = operand_of[("classes", group // GROUPS)]
+            product_of[group] = []
             for first in range(0, GROUP, BANK_TILES):
-                acc = psum_out.tile([P, BANK_TILES, CLASSES], F32)
+                acc = psum_scalar.tile([P, BANK_TILES, CLASSES], F32, tag="bank")
+                product_of[group].append(acc)
                 for i in range(BANK_TILES):
                     samples = slice((first + i) * P, (first + i + 1) * P)
                     nc.tensor.matmul_mx(
                         out=acc[:, i, :],
                         lhsT=codes[:, samples].bitcast(FP8X4),
                         lhsT_scale=plane[:, samples],
-                        rhs=fc_codes[:, n, :].bitcast(FP8X4),
-                        rhs_scale=fc_planes[:, n, :],
+                        rhs=class_codes.bitcast(FP8X4),
+                        rhs_scale=class_plane,
                         start=True,
                         stop=True,
                     )
-                nc.scalar.copy(out=logits[:, first : first + BANK_TILES, :], in_=acc[:])
-            nc.scalar.dma_start(out=out_tiles[:, g * GROUP : (g + 1) * GROUP, n, :], in_=logits[:])
 
-        def classifier_norm_stage(n):
-            fc_t = classifier.tile([P, PACK, CLASSES], F32)
-            fc_columns_of[n] = fc_t
-            nc.scalar.copy(out=fc_t[:], in_=fc_raw[:, n * HALVES : (n + 1) * HALVES, :].rearrange("p u (e k) -> p (u e) k", e=PAIR))
-            fc_inverse_of[n] = inverse_column_norms(fc_t, CLASS_TILES)
+        def leave_stage(group):
+            n, g = divmod(group, GROUPS)
+            logits = results.tile([P, GROUP, CLASSES], F32)
+            for i, acc in enumerate(product_of[group]):
+                nc.scalar.copy(out=logits[:, i * BANK_TILES : (i + 1) * BANK_TILES, :], in_=acc[:])
+            nc.sync.dma_start(out=out_tiles[:, g * GROUP : (g + 1) * GROUP, n, :], in_=logits[:])
 
-        def classifier_scale_stage(n):
-            scale_columns_and_quantise(fc_columns_of[n], fc_inverse_of[n], CLASS_TILES, fc_codes[:, n, :], fc_planes[:, n, :])
+        for group in range(LOAD_LEAD):
+            load_stage(group)
+        for step in range(LAST_STEP + 1):
+            if is_group(step + LOAD_LEAD):
+                load_stage(step + LOAD_LEAD)
 
-        for step in range(all_groups + MATMUL_LAG):
-            if 0 <= step - MATMUL_LAG:
-                matmul_stage(step - MATMUL_LAG)
-            if 0 <= step - SCALE_LAG < all_groups:
-                scale_stage(step - SCALE_LAG)
-            if 0 <= step - NORM_LAG < all_groups:
-                norm_stage(step - NORM_LAG)
-            if 0 <= step - AFFINE_LAG < all_groups:
+            for key in columns_due(step - NORM_AFTER):
+                clamp_stage(key)
+            if step == SMALL_INPUTS_STEP + 1:
+                keep_gamma_and_beta()
+            if is_group(step - STATS_LAG):
+                statistics_stage(step - STATS_LAG, 0)
+            for key in columns_due(step - INVERSE_AFTER):
+                inverse_stage(key)
+            for n in bin_due(step, COEFFICIENTS_LAG):
+                coefficients_stage(n)
+            for key in columns_due(step - SCALE_AFTER):
+                scale_stage(key)
+            if is_group(step - STATS_LAG):
+                statistics_stage(step - STATS_LAG, 1)
+            for key in columns_due(step - SCALE_AFTER):
+                quantise_stage(key)
+            for n in bin_due(step, MOMENTS_LAG):
+                moments_stage(n)
+
+            if is_group(step - AFFINE_LAG):
                 affine_stage(step - AFFINE_LAG)
-            if step < 2 * BINS and step % 2 == 1:
-                classifier_scale_stage(step // 2)
-            if step < 2 * BINS and step % 2 == 0:
-                classifier_norm_stage(step // 2)
-            if step < all_groups:
-                statistics_stage(step)
-                if step % GROUPS == GROUPS - 1:
-                    coefficients(step // GROUPS)
+
+            for key in columns_due(step):
+                if key[0] == "classes":
+                    classifier_cast(key[1])
+                squares_stage(key)
+            if is_group(step - SQUARES_LAG - MATMUL_AFTER):
+                matmul_stage(step - SQUARES_LAG - MATMUL_AFTER)
+                leave_stage(step - SQUARES_LAG - MATMUL_AFTER)
+            if is_group(step):
+                turn_stage(step)
+
+            for key in columns_due(step - INVERSE_AFTER):
+                spread_stage(key)
+            if step == SMALL_INPUTS_STEP:
+                turn_gamma_and_beta()
+            for key in columns_due(step - NORM_AFTER):
+                norm_stage(key)
+            for n in bin_due(step, DEVIATION_LAG):
+                deviation_stage(n)

@@ -49,6 +49,7 @@ MATMUL_AFTER = 4
 SMALL_INPUTS_STEP = 2
 LAST_STEP = ALL_GROUPS - 1 + SQUARES_LAG + MATMUL_AFTER
 
+GPSIMD_ROWS = 3
 SCALAR_BANKS = 6
 SPREAD_BANKS = 2
 
@@ -184,9 +185,12 @@ def tile_gmpahead_pb_t_kernel(tc, emb, gamma, beta, fc1d, out):
                 values = turned_of[group][:, u * COLS : (u + 1) * COLS].bitcast(BF16).rearrange("p (c e) -> p c e", e=PAIR)
                 for e in range(PAIR):
                     t = PAIR * u + e
-                    nc.gpsimd.tensor_scalar(
-                        out=y_t[:, t, :], in0=values[:, :, e], scalar1=gain[:, t : t + 1], scalar2=shift[:, t : t + 1], op0=ALU.mult, op1=ALU.add
-                    )
+                    if t < GPSIMD_ROWS:
+                        nc.gpsimd.tensor_scalar(
+                            out=y_t[:, t, :], in0=values[:, :, e], scalar1=gain[:, t : t + 1], scalar2=shift[:, t : t + 1], op0=ALU.mult, op1=ALU.add
+                        )
+                    else:
+                        nc.scalar.activation(out=y_t[:, t, :], in_=values[:, :, e], func=ACT.Identity, scale=gain[:, t : t + 1], bias=shift[:, t : t + 1])
 
         def classifier_cast(n):
             fc_t = classifier.tile([P, PACK, CLASSES], F32)

@@ -49,6 +49,7 @@ MATMUL_AFTER = 4
 SMALL_INPUTS_STEP = 2
 LAST_STEP = ALL_GROUPS - 1 + SQUARES_LAG + MATMUL_AFTER
 
+RUN = 4
 GPSIMD_ROWS = 3
 SCALAR_BANKS = 6
 SPREAD_BANKS = 2
@@ -250,9 +251,9 @@ def tile_gmpahead_pb_t_kernel(tc, emb, gamma, beta, fc1d, out):
             grouped = quant.tile([P, COLS, PACK], BF16, align_bytes=64)
             grouped_of[key] = grouped
             nc.vector.tensor_tensor(
-                out=grouped[:, 0:cols, :],
-                in0=columns_of[key].rearrange("p t c -> p c t"),
-                in1=spread_of[key][:, 0:cols].unsqueeze(2).to_broadcast([P, cols, PACK]),
+                out=grouped[:, 0:cols, :].rearrange("p (c i) t -> p c t i", i=RUN),
+                in0=columns_of[key].rearrange("p t (c i) -> p c t i", i=RUN),
+                in1=spread_of[key][:, 0:cols].rearrange("p (c i) -> p c i", i=RUN).unsqueeze(2).to_broadcast([P, cols // RUN, PACK, RUN]),
                 op=ALU.mult,
             )
 

@@ -38,19 +38,16 @@ FLOPS = 2 * BINS * SAMPLES * FEATURES * CLASSES
 LOAD_LEAD = 3
 STATS_LAG = 1
 MOMENTS_LAG = GROUPS - 1 + STATS_LAG
-DEVIATION_LAG = MOMENTS_LAG + 1
-COEFFICIENTS_LAG = DEVIATION_LAG + 1
+COEFFICIENTS_LAG = MOMENTS_LAG + 1
 AFFINE_LAG = COEFFICIENTS_LAG + 1
 SQUARES_LAG = AFFINE_LAG + 1
-NORM_AFTER = 1
-INVERSE_AFTER = 2
-SCALE_AFTER = 3
-MATMUL_AFTER = 4
+SCALE_AFTER = 1
+QUANTISE_AFTER = 2
+MATMUL_AFTER = 2
 SMALL_INPUTS_STEP = 2
 LAST_STEP = ALL_GROUPS - 1 + SQUARES_LAG + MATMUL_AFTER
 
 RUN = 4
-GPSIMD_ROWS = 3
 SCALAR_BANKS = 6
 SPREAD_BANKS = 2
 
@@ -98,8 +95,6 @@ def tile_gmpahead_pb_t_kernel(tc, emb, gamma, beta, fc1d, out):
         gb_bank = {}
         columns_of = {}
         norm_sq_of = {}
-        clamped_of = {}
-        norm_of = {}
         inverse_of = {}
         spread_of = {}
         grouped_of = {}
@@ -158,22 +153,18 @@ def tile_gmpahead_pb_t_kernel(tc, emb, gamma, beta, fc1d, out):
             for u in range(HALVES):
                 for e in range(PAIR):
                     nc.vector.bn_aggr(out=moments[:, PAIR * u + e, :], in_=stats_of[n][:, u, :, 3 * e : 3 * e + 3])
-            var_eps = per_bin.tile([P, PACK], F32)
-            nc.vector.tensor_scalar_add(out=var_eps[:], in0=moments[:, :, 1], scalar1=BN_EPS)
-            moments_of[n] = (moments, var_eps)
+            moments_of[n] = moments
 
         def deviation_stage(n):
-            std = per_bin.tile([P, PACK], F32)
-            deviation_of[n] = std
-            nc.scalar.sqrt(out=std[:], in_=moments_of[n][1][:])
+            rstd = per_bin.tile([P, PACK], F32)
+            deviation_of[n] = rstd
+            nc.scalar.activation(out=rstd[:], in_=moments_of[n][:, :, 1], func=ACT.Abs_reciprocal_sqrt, bias=BN_EPS)
 
         def coefficients_stage(n):
-            rstd = per_bin.tile([P, PACK], F32)
-            nc.vector.reciprocal(out=rstd[:], in_=deviation_of[n][:])
             gain = per_bin.tile([P, PACK], F32)
-            nc.vector.tensor_mul(out=gain[:], in0=gb_t[:, n, :], in1=rstd[:])
+            nc.vector.tensor_mul(out=gain[:], in0=gb_t[:, n, :], in1=deviation_of[n][:])
             gain_mean = per_bin.tile([P, PACK], F32)
-            nc.vector.tensor_mul(out=gain_mean[:], in0=gain[:], in1=moments_of[n][0][:, :, 0])
+            nc.vector.tensor_mul(out=gain_mean[:], in0=gain[:], in1=moments_of[n][:, :, 0])
             shift = per_bin.tile([P, PACK], F32)
             nc.vector.tensor_sub(out=shift[:], in0=gb_t[:, BINS + n, :], in1=gain_mean[:])
             coefficients_of[n] = (gain, shift)
@@ -186,12 +177,9 @@ def tile_gmpahead_pb_t_kernel(tc, emb, gamma, beta, fc1d, out):
                 values = turned_of[group][:, u * COLS : (u + 1) * COLS].bitcast(BF16).rearrange("p (c e) -> p c e", e=PAIR)
                 for e in range(PAIR):
                     t = PAIR * u + e
-                    if t < GPSIMD_ROWS:
-                        nc.gpsimd.tensor_scalar(
-                            out=y_t[:, t, :], in0=values[:, :, e], scalar1=gain[:, t : t + 1], scalar2=shift[:, t : t + 1], op0=ALU.mult, op1=ALU.add
-                        )
-                    else:
-                        nc.scalar.activation(out=y_t[:, t, :], in_=values[:, :, e], func=ACT.Identity, scale=gain[:, t : t + 1], bias=shift[:, t : t + 1])
+                    nc.gpsimd.tensor_scalar(
+                        out=y_t[:, t, :], in0=values[:, :, e], scalar1=gain[:, t : t + 1], scalar2=shift[:, t : t + 1], op0=ALU.mult, op1=ALU.add
+                    )
 
         def classifier_cast(n):
             fc_t = classifier.tile([P, PACK, CLASSES], F32)
@@ -222,23 +210,11 @@ def tile_gmpahead_pb_t_kernel(tc, emb, gamma, beta, fc1d, out):
                 squares = scrap.tile([P, PACK * P], BF16)
                 nc.scalar.activation(out=squares[:], in_=back[:], func=ACT.Square, accum_out=norm_sq[:, j : j + 1])
 
-        def clamp_stage(key):
-            tiles = tiles_of(key)
-            clamped = small.tile([P, GROUP], F32)
-            clamped_of[key] = clamped
-            nc.vector.tensor_scalar_max(out=clamped[:, 0:tiles], in0=norm_sq_of[key][:, 0:tiles], scalar1=L2_EPS * L2_EPS)
-
-        def norm_stage(key):
-            tiles = tiles_of(key)
-            norm = small.tile([P, GROUP], F32)
-            norm_of[key] = norm
-            nc.scalar.sqrt(out=norm[:, 0:tiles], in_=clamped_of[key][:, 0:tiles])
-
         def inverse_stage(key):
             tiles = tiles_of(key)
             inverse = small.tile([P, GROUP], F32)
             inverse_of[key] = inverse
-            nc.vector.reciprocal(out=inverse[:, 0:tiles], in_=norm_of[key][:, 0:tiles])
+            nc.scalar.activation(out=inverse[:, 0:tiles], in_=norm_sq_of[key][:, 0:tiles], func=ACT.Abs_reciprocal_sqrt, bias=L2_EPS * L2_EPS)
 
         def spread_stage(key):
             spread = psum_spread.tile([P, COLS], F32)
@@ -289,11 +265,14 @@ def tile_gmpahead_pb_t_kernel(tc, emb, gamma, beta, fc1d, out):
                         stop=True,
                     )
 
-        def leave_stage(group):
+        def leave_stage(group, between):
             n, g = divmod(group, GROUPS)
             logits = results.tile([P, GROUP, CLASSES], F32)
             for i, acc in enumerate(product_of[group]):
                 nc.scalar.copy(out=logits[:, i * BANK_TILES : (i + 1) * BANK_TILES, :], in_=acc[:])
+                if i == 0:
+                    for key in between:
+                        inverse_stage(key)
             nc.sync.dma_start(out=out_tiles[:, g * GROUP : (g + 1) * GROUP, n, :], in_=logits[:])
 
         for group in range(LOAD_LEAD):
@@ -302,43 +281,42 @@ def tile_gmpahead_pb_t_kernel(tc, emb, gamma, beta, fc1d, out):
             if is_group(step + LOAD_LEAD):
                 load_stage(step + LOAD_LEAD)
 
-            for key in columns_due(step - NORM_AFTER):
-                clamp_stage(key)
+            for n in bin_due(step, COEFFICIENTS_LAG):
+                deviation_stage(n)
+
+            for key in columns_due(step - QUANTISE_AFTER):
+                quantise_stage(key)
             if step == SMALL_INPUTS_STEP + 1:
                 keep_gamma_and_beta()
             if is_group(step - STATS_LAG):
                 statistics_stage(step - STATS_LAG, 0)
-            for key in columns_due(step - INVERSE_AFTER):
-                inverse_stage(key)
             for n in bin_due(step, COEFFICIENTS_LAG):
                 coefficients_stage(n)
             for key in columns_due(step - SCALE_AFTER):
                 scale_stage(key)
             if is_group(step - STATS_LAG):
                 statistics_stage(step - STATS_LAG, 1)
-            for key in columns_due(step - SCALE_AFTER):
-                quantise_stage(key)
             for n in bin_due(step, MOMENTS_LAG):
                 moments_stage(n)
 
             if is_group(step - AFFINE_LAG):
                 affine_stage(step - AFFINE_LAG)
 
-            for key in columns_due(step):
+            keys = columns_due(step)
+            for key in keys:
                 if key[0] == "classes":
                     classifier_cast(key[1])
                 squares_stage(key)
             if is_group(step - SQUARES_LAG - MATMUL_AFTER):
                 matmul_stage(step - SQUARES_LAG - MATMUL_AFTER)
-                leave_stage(step - SQUARES_LAG - MATMUL_AFTER)
+                leave_stage(step - SQUARES_LAG - MATMUL_AFTER, keys)
+                keys = []
             if is_group(step):
                 turn_stage(step)
+            for key in keys:
+                inverse_stage(key)
 
-            for key in columns_due(step - INVERSE_AFTER):
+            for key in columns_due(step):
                 spread_stage(key)
             if step == SMALL_INPUTS_STEP:
                 turn_gamma_and_beta()
-            for key in columns_due(step - NORM_AFTER):
-                norm_stage(key)
-            for n in bin_due(step, DEVIATION_LAG):
-                deviation_stage(n)

@@ -37,18 +37,25 @@ FLOPS = 2 * BINS * SAMPLES * FEATURES * CLASSES
 
 LOAD_LEAD = 3
 STATS_LAG = 1
+FILL = 1
 MOMENTS_LAG = GROUPS - 1 + STATS_LAG
 COEFFICIENTS_LAG = MOMENTS_LAG + 1
-AFFINE_LAG = COEFFICIENTS_LAG + 1
+AFFINE_LAG = COEFFICIENTS_LAG + FILL
 SQUARES_LAG = AFFINE_LAG + 1
 SCALE_AFTER = 1
 QUANTISE_AFTER = 2
 MATMUL_AFTER = 2
 SMALL_INPUTS_STEP = 2
+CLASSES_STEP = 3
+CLASSES_SCALE_AFTER = 2
 LAST_STEP = ALL_GROUPS - 1 + SQUARES_LAG + MATMUL_AFTER
 
+GRAM_BIN = 0
+GRAM_GROUPS = (0, 2, 4, 6)
+
 RUN = 4
-SCALAR_BANKS = 6
+TURN_BANKS = 2
+SCALAR_BANKS = 4
 SPREAD_BANKS = 2
 
 
@@ -59,21 +66,26 @@ def tile_gmpahead_pb_t_kernel(tc, emb, gamma, beta, fc1d, out):
 
     with ExitStack() as stack:
         const = stack.enter_context(tc.tile_pool(name="const", bufs=1))
-        loads = stack.enter_context(tc.tile_pool(name="loads", bufs=LOAD_LEAD + 2))
+        loads = stack.enter_context(tc.tile_pool(name="loads", bufs=LOAD_LEAD + GROUPS))
         turned = stack.enter_context(tc.tile_pool(name="turned", bufs=AFFINE_LAG + 2))
         columns = stack.enter_context(tc.tile_pool(name="columns", bufs=SQUARES_LAG - AFFINE_LAG + SCALE_AFTER + 2))
-        classifier = stack.enter_context(tc.tile_pool(name="classifier", bufs=SCALE_AFTER + 1))
         small = stack.enter_context(tc.tile_pool(name="small", bufs=4))
         per_bin = stack.enter_context(tc.tile_pool(name="per_bin", bufs=2))
         scrap = stack.enter_context(tc.tile_pool(name="scrap", bufs=4))
         quant = stack.enter_context(tc.tile_pool(name="quant", bufs=3))
         results = stack.enter_context(tc.tile_pool(name="results", bufs=4))
+        psum_turn = stack.enter_context(tc.psum_pool(name="psum_turn", bufs=TURN_BANKS))
         psum_scalar = stack.enter_context(tc.psum_pool(name="psum_scalar", bufs=SCALAR_BANKS))
         psum_spread = stack.enter_context(tc.psum_pool(name="psum_spread", bufs=SPREAD_BANKS))
         stack.enter_context(tc.manual_schedule())
 
         ident = const.tile([P, P], F32)
         make_identity(nc, ident[:])
+        ident_bf = const.tile([P, P], BF16)
+        make_identity(nc, ident_bf[:])
+
+        ones = const.tile([P, 1], BF16)
+        nc.vector.memset(ones[:], 1.0)
 
         gb_rows = const.tile([P, HALVES * P], F32)
         nc.vector.memset(gb_rows[:], 0.0)
@@ -81,19 +93,26 @@ def tile_gmpahead_pb_t_kernel(tc, emb, gamma, beta, fc1d, out):
         nc.scalar.dma_start(out=gb_rows[BINS : 2 * BINS, :].bitcast(BF16), in_=beta)
         gb_t = const.tile([P, 2 * BINS, PACK], F32)
         fc_raw = const.tile([P, BINS * HALVES, PAIR * CLASSES], BF16)
-        nc.scalar.dma_start(out=fc_raw[:], in_=fc1d.rearrange("n (u p e) k -> p (n u) (e k)", u=HALVES, e=PAIR))
         fc_codes = const.tile([P, BINS, CLASSES], U32, align_bytes=64)
         fc_planes = const.tile([P, BINS, CLASSES], U8, align_bytes=64)
 
         loaded_of = {}
         turned_of = {}
         stats_of = {}
+        first_slot_of = {}
         moments_of = {}
         deviation_of = {}
         coefficients_of = {}
         product_of = {}
+        logits_of = {}
+        gram_banks = []
+        parts_of = {}
+        squares_of = {}
+        sums_of = {}
         gb_bank = {}
         columns_of = {}
+        for n in range(BINS):
+            columns_of[("classes", n)] = fc_raw[:, n * HALVES : (n + 1) * HALVES, :].rearrange("p u (e k) -> p (u e) k", e=PAIR)
         norm_sq_of = {}
         inverse_of = {}
         spread_of = {}
@@ -114,9 +133,11 @@ def tile_gmpahead_pb_t_kernel(tc, emb, gamma, beta, fc1d, out):
             keys = []
             if is_group(step - SQUARES_LAG):
                 keys.append(("samples", step - SQUARES_LAG))
-            if is_bin(step - SMALL_INPUTS_STEP):
-                keys.append(("classes", step - SMALL_INPUTS_STEP))
             return keys
+
+        def classes_due(step):
+            n, rest = divmod(step - CLASSES_STEP, 2)
+            return [("classes", n)] if rest == 0 and is_bin(n) else []
 
         def tiles_of(key):
             return GROUP if key[0] == "samples" else CLASS_TILES
@@ -126,33 +147,114 @@ def tile_gmpahead_pb_t_kernel(tc, emb, gamma, beta, fc1d, out):
             n, g = divmod(group, GROUPS)
             raw = loads.tile([P, GROUP * FEATURES], BF16)
             loaded_of[group] = raw
-            nc.sync.dma_start(out=raw[:].rearrange("p (j o) -> p j o", j=GROUP), in_=emb_tiles[n, :, g * GROUP : (g + 1) * GROUP, :])
+            pieces = 2 if group == 0 else 1
+            tiles = GROUP // pieces
+            for piece in range(pieces):
+                nc.sync.dma_start(
+                    out=raw[:, piece * tiles * FEATURES : (piece + 1) * tiles * FEATURES].rearrange("p (j o) -> p j o", j=tiles),
+                    in_=emb_tiles[n, :, g * GROUP + piece * tiles : g * GROUP + (piece + 1) * tiles, :],
+                )
 
         def turn_stage(group):
             words = loaded_of[group][:].bitcast(F32)
             e_t = turned.tile([P, HALVES * COLS], F32)
             turned_of[group] = e_t
             for u in range(HALVES):
-                bank = psum_scalar.tile([P, COLS], F32, tag="bank")
+                bank = psum_turn.tile([P, COLS], F32, tag="bank")
                 for j in range(GROUP):
                     first = (j * HALVES + u) * P
                     nc.tensor.transpose(out=bank[:, j * P : (j + 1) * P], in_=words[:, first : first + P], identity=ident[:])
                 nc.scalar.copy(out=e_t[:, u * COLS : (u + 1) * COLS], in_=bank[:])
 
-        def statistics_stage(group, u):
+        def is_gram(group):
             n, g = divmod(group, GROUPS)
-            if g == 0 and u == 0:
-                stats = per_bin.tile([P, HALVES, GROUPS * CHUNKS, STATS], F32)
+            return n == GRAM_BIN and g in GRAM_GROUPS
+
+        def features_of(group, t, j):
+            u, e = divmod(t, PAIR)
+            return loaded_of[group][:].rearrange("p (j u q e) -> p j u e q", j=GROUP, u=HALVES, e=PAIR)[:, j, u, e, :]
+
+        def summed_part(n):
+            if n == GRAM_BIN:
+                return range(PACK), [(n * GROUPS + g, j) for g in GRAM_GROUPS for j in range(GROUP)]
+            return range(PACK - PAIR, PACK), [(n * GROUPS + g, j) for g in range(GROUPS) for j in range(GROUP // CHUNKS, GROUP)]
+
+        def gram_stage(group):
+            if group % GROUPS == GRAM_GROUPS[0]:
+                for t in range(PACK):
+                    bank = psum_scalar.tile([P, P], F32, tag="bank")
+                    gram_banks.append(bank)
+            for t in range(PACK):
+                for j in range(GROUP):
+                    some = features_of(group, t, j)
+                    tiles = summed_part(GRAM_BIN)[1]
+                    nc.tensor.matmul(out=gram_banks[t][:], lhsT=some, rhs=some, start=(group, j) == tiles[0], stop=(group, j) == tiles[-1])
+
+        def gram_squares_stage():
+            squares = per_bin.tile([P, PACK], F32)
+            squares_of[GRAM_BIN] = squares[:]
+            for t in range(PACK):
+                diagonal = scrap.tile([P, P], F32)
+                nc.vector.scalar_tensor_tensor(
+                    out=diagonal[:], in0=gram_banks[t][:], scalar=1.0, in1=ident[:], op0=ALU.mult, op1=ALU.mult, accum_out=squares[:, t : t + 1]
+                )
+
+        def scalar_squares_stage(group):
+            n, g = divmod(group, GROUPS)
+            if g == 0:
+                parts = per_bin.tile([P, PAIR, GROUPS], F32)
+                parts_of[n] = parts
+            chunk = turned_of[group][:, HALVES * COLS - BN_CHUNK // PAIR :].bitcast(BF16).rearrange("p (c e) -> p e c", e=PAIR)
+            for e in range(PAIR):
+                junk = scrap.tile([P, BN_CHUNK // PAIR], BF16)
+                nc.scalar.activation(out=junk[:], in_=chunk[:, e, :], func=ACT.Square, accum_out=parts_of[n][:, e, g : g + 1])
+
+        def sums_stage(n):
+            rows, tiles = summed_part(n)
+            spread = psum_spread.tile([P, PACK], F32, tag="spread")
+            sums_of[n] = spread[:, rows[0] : rows[-1] + 1]
+            for t in rows:
+                for group, j in tiles:
+                    nc.tensor.matmul(
+                        out=spread[:, t : t + 1], lhsT=features_of(group, t, j), rhs=ones[:], start=(group, j) == tiles[0], stop=(group, j) == tiles[-1]
+                    )
+
+        def summed_statistics_stage(n):
+            rows, tiles = summed_part(n)
+            samples = len(tiles) * P
+            first = rows[0] // PAIR
+            if n != GRAM_BIN:
+                squares = per_bin.tile([P, PAIR], F32)
+                squares_of[n] = squares[:]
+                nc.vector.reduce_sum(out=squares[:], in_=parts_of[n][:], axis=mybir.AxisListType.X)
+            pairs = "p (u e) -> p u e"
+            sums = sums_of[n].rearrange(pairs, e=PAIR)
+            slots = stats_of[n][:, first:, GROUPS * CHUNKS, :].rearrange("p u (e s) -> p u e s", e=PAIR)
+            nc.vector.memset(slots[:, :, :, 0], float(samples))
+            nc.vector.tensor_scalar_mul(out=slots[:, :, :, 1], in0=sums, scalar1=1.0 / samples)
+            sum_mean = per_bin.tile([P, HALVES, PAIR], F32)
+            nc.vector.tensor_mul(out=sum_mean[:, first:, :], in0=sums, in1=slots[:, :, :, 1])
+            nc.vector.tensor_sub(out=slots[:, :, :, 2], in0=squares_of[n].rearrange(pairs, e=PAIR), in1=sum_mean[:, first:, :])
+
+        def statistics_stage(group, u):
+            n = group // GROUPS
+            if n not in stats_of:
+                stats = per_bin.tile([P, HALVES, GROUPS * CHUNKS + 1, STATS], F32)
                 stats_of[n] = stats
+                first_slot_of[n] = [GROUPS * CHUNKS] * HALVES
             values = turned_of[group][:, u * COLS : (u + 1) * COLS].bitcast(BF16)
             for h in range(CHUNKS):
-                nc.vector.bn_stats(out=stats_of[n][:, u, g * CHUNKS + h, :], in_=values[:, h * BN_CHUNK : (h + 1) * BN_CHUNK])
+                if n != GRAM_BIN and (u, h) == (HALVES - 1, CHUNKS - 1):
+                    continue
+                first_slot_of[n][u] -= 1
+                nc.vector.bn_stats(out=stats_of[n][:, u, first_slot_of[n][u], :], in_=values[:, h * BN_CHUNK : (h + 1) * BN_CHUNK])
 
         def moments_stage(n):
             moments = per_bin.tile([P, PACK, 2], F32)
             for u in range(HALVES):
+                last = GROUPS * CHUNKS + (PAIR * u in summed_part(n)[0])
                 for e in range(PAIR):
-                    nc.vector.bn_aggr(out=moments[:, PAIR * u + e, :], in_=stats_of[n][:, u, :, 3 * e : 3 * e + 3])
+                    nc.vector.bn_aggr(out=moments[:, PAIR * u + e, :], in_=stats_of[n][:, u, first_slot_of[n][u] : last, 3 * e : 3 * e + 3])
             moments_of[n] = moments
 
         def deviation_stage(n):
@@ -172,7 +274,7 @@ def tile_gmpahead_pb_t_kernel(tc, emb, gamma, beta, fc1d, out):
         def affine_stage(group):
             gain, shift = coefficients_of[group // GROUPS]
             y_t = columns.tile([P, PACK, COLS], F32)
-            columns_of[("samples", group)] = y_t
+            columns_of[("samples", group)] = y_t[:]
             for u in range(HALVES):
                 values = turned_of[group][:, u * COLS : (u + 1) * COLS].bitcast(BF16).rearrange("p (c e) -> p c e", e=PAIR)
                 for e in range(PAIR):
@@ -181,13 +283,8 @@ def tile_gmpahead_pb_t_kernel(tc, emb, gamma, beta, fc1d, out):
                         out=y_t[:, t, :], in0=values[:, :, e], scalar1=gain[:, t : t + 1], scalar2=shift[:, t : t + 1], op0=ALU.mult, op1=ALU.add
                     )
 
-        def classifier_cast(n):
-            fc_t = classifier.tile([P, PACK, CLASSES], F32)
-            columns_of[("classes", n)] = fc_t
-            nc.scalar.copy(out=fc_t[:], in_=fc_raw[:, n * HALVES : (n + 1) * HALVES, :].rearrange("p u (e k) -> p (u e) k", e=PAIR))
-
         def turn_gamma_and_beta():
-            spread = psum_spread.tile([P, COLS], F32)
+            spread = psum_spread.tile([P, COLS], F32, tag="spread")
             gb_bank[0] = spread
             for u in range(HALVES):
                 nc.tensor.transpose(out=spread[:, u * P : (u + 1) * P], in_=gb_rows[:, u * P : (u + 1) * P], identity=ident[:])
@@ -199,16 +296,23 @@ def tile_gmpahead_pb_t_kernel(tc, emb, gamma, beta, fc1d, out):
             )
 
 
-        def squares_stage(key):
+        def squares_stage(key, tiles):
             x_t = columns_of[key]
-            norm_sq = small.tile([P, GROUP], F32)
-            norm_sq_of[key] = norm_sq
-            for j in range(tiles_of(key)):
-                back = psum_scalar.tile([P, PACK * P], F32, tag="bank")
+            samples = key[0] == "samples"
+            if key not in norm_sq_of:
+                norm_sq = small.tile([P, GROUP], F32)
+                norm_sq_of[key] = norm_sq
+            for j in tiles:
+                if samples:
+                    back = psum_scalar.tile([P, PACK * P], F32, tag="bank")
+                else:
+                    back = psum_spread.tile([P, PACK * P], BF16, tag="spread")
                 for t in range(PACK):
-                    nc.tensor.transpose(out=back[:, t * P : (t + 1) * P], in_=x_t[:, t, j * P : (j + 1) * P], identity=ident[:])
+                    nc.tensor.transpose(
+                        out=back[:, t * P : (t + 1) * P], in_=x_t[:, t, j * P : (j + 1) * P], identity=ident[:] if samples else ident_bf[:]
+                    )
                 squares = scrap.tile([P, PACK * P], BF16)
-                nc.scalar.activation(out=squares[:], in_=back[:], func=ACT.Square, accum_out=norm_sq[:, j : j + 1])
+                nc.scalar.activation(out=squares[:], in_=back[:], func=ACT.Square, accum_out=norm_sq_of[key][:, j : j + 1])
 
         def inverse_stage(key):
             tiles = tiles_of(key)
@@ -217,7 +321,7 @@ def tile_gmpahead_pb_t_kernel(tc, emb, gamma, beta, fc1d, out):
             nc.scalar.activation(out=inverse[:, 0:tiles], in_=norm_sq_of[key][:, 0:tiles], func=ACT.Abs_reciprocal_sqrt, bias=L2_EPS * L2_EPS)
 
         def spread_stage(key):
-            spread = psum_spread.tile([P, COLS], F32)
+            spread = psum_spread.tile([P, COLS], F32, tag="spread")
             spread_of[key] = spread
             for j in range(tiles_of(key)):
                 nc.tensor.transpose(out=spread[:, j * P : (j + 1) * P], in_=inverse_of[key][:, j : j + 1].to_broadcast([P, P]), identity=ident[:])
@@ -264,19 +368,18 @@ def tile_gmpahead_pb_t_kernel(tc, emb, gamma, beta, fc1d, out):
                         start=True,
                         stop=True,
                     )
-
-        def leave_stage(group, between):
-            n, g = divmod(group, GROUPS)
             logits = results.tile([P, GROUP, CLASSES], F32)
-            for i, acc in enumerate(product_of[group]):
-                nc.scalar.copy(out=logits[:, i * BANK_TILES : (i + 1) * BANK_TILES, :], in_=acc[:])
-                if i == 0:
-                    for key in between:
-                        inverse_stage(key)
-            nc.sync.dma_start(out=out_tiles[:, g * GROUP : (g + 1) * GROUP, n, :], in_=logits[:])
+            logits_of[group] = logits
+
+        def leave_stage(group, half):
+            n, g = divmod(group, GROUPS)
+            nc.scalar.copy(out=logits_of[group][:, half * BANK_TILES : (half + 1) * BANK_TILES, :], in_=product_of[group][half][:])
+            if half == GROUP // BANK_TILES - 1:
+                nc.sync.dma_start(out=out_tiles[:, g * GROUP : (g + 1) * GROUP, n, :], in_=logits_of[group][:])
 
         for group in range(LOAD_LEAD):
             load_stage(group)
+        nc.sync.dma_start(out=fc_raw[:], in_=fc1d.rearrange("n (u p e) k -> p (n u) (e k)", u=HALVES, e=PAIR))
         for step in range(LAST_STEP + 1):
             if is_group(step + LOAD_LEAD):
                 load_stage(step + LOAD_LEAD)
@@ -284,39 +387,53 @@ def tile_gmpahead_pb_t_kernel(tc, emb, gamma, beta, fc1d, out):
             for n in bin_due(step, COEFFICIENTS_LAG):
                 deviation_stage(n)
 
-            for key in columns_due(step - QUANTISE_AFTER):
+            for key in columns_due(step - QUANTISE_AFTER) + classes_due(step - CLASSES_SCALE_AFTER - 1):
                 quantise_stage(key)
             if step == SMALL_INPUTS_STEP + 1:
                 keep_gamma_and_beta()
-            if is_group(step - STATS_LAG):
+            bn_group = is_group(step - STATS_LAG) and not is_gram(step - STATS_LAG)
+            if bn_group:
                 statistics_stage(step - STATS_LAG, 0)
             for n in bin_due(step, COEFFICIENTS_LAG):
                 coefficients_stage(n)
-            for key in columns_due(step - SCALE_AFTER):
+
+            turn, square, product = step, step - SQUARES_LAG, step - SQUARES_LAG - MATMUL_AFTER
+            if is_group(square):
+                squares_stage(("samples", square), range(0, GROUP // 2))
+            for key in columns_due(step - SCALE_AFTER) + classes_due(step - CLASSES_SCALE_AFTER):
+                spread_stage(key)
+            if is_group(square):
+                squares_stage(("samples", square), range(GROUP // 2, GROUP))
+            if is_group(product):
+                matmul_stage(product)
+                leave_stage(product, 0)
+            if is_group(square):
+                inverse_stage(("samples", square))
+            if is_group(product):
+                leave_stage(product, 1)
+            if is_group(step - STATS_LAG) and (step - STATS_LAG) // GROUPS != GRAM_BIN:
+                scalar_squares_stage(step - STATS_LAG)
+            if is_group(turn):
+                turn_stage(turn)
+                if is_gram(turn):
+                    gram_stage(turn)
+            for n in bin_due(step, GROUPS - 1):
+                sums_stage(n)
+            if step == SMALL_INPUTS_STEP:
+                turn_gamma_and_beta()
+            for key in classes_due(step):
+                squares_stage(key, range(CLASS_TILES))
+                inverse_stage(key)
+
+            for key in columns_due(step - SCALE_AFTER) + classes_due(step - CLASSES_SCALE_AFTER):
                 scale_stage(key)
-            if is_group(step - STATS_LAG):
+            if bn_group:
                 statistics_stage(step - STATS_LAG, 1)
+            if step == GRAM_BIN * GROUPS + GRAM_GROUPS[-1] + STATS_LAG:
+                gram_squares_stage()
             for n in bin_due(step, MOMENTS_LAG):
+                summed_statistics_stage(n)
                 moments_stage(n)
 
             if is_group(step - AFFINE_LAG):
                 affine_stage(step - AFFINE_LAG)
-
-            keys = columns_due(step)
-            for key in keys:
-                if key[0] == "classes":
-                    classifier_cast(key[1])
-                squares_stage(key)
-            if is_group(step - SQUARES_LAG - MATMUL_AFTER):
-                matmul_stage(step - SQUARES_LAG - MATMUL_AFTER)
-                leave_stage(step - SQUARES_LAG - MATMUL_AFTER, keys)
-                keys = []
-            if is_group(step):
-                turn_stage(step)
-            for key in keys:
-                inverse_stage(key)
-
-            for key in columns_due(step):
-                spread_stage(key)
-            if step == SMALL_INPUTS_STEP:
-                turn_gamma_and_beta()

@@ -52,7 +52,9 @@ LAST_STEP = ALL_GROUPS - 1 + SQUARES_LAG + MATMUL_AFTER
 
 GRAM_BIN = 0
 GRAM_GROUPS = (0, 2, 4, 6)
+SCALAR_GROUPS = (1, 2, 3, 5, 6, 7)
 
+SHARED_GPSIMD_ROWS = 2
 RUN = 4
 TURN_BANKS = 2
 SCALAR_BANKS = 4
@@ -170,6 +172,10 @@ def tile_gmpahead_pb_t_kernel(tc, emb, gamma, beta, fc1d, out):
             n, g = divmod(group, GROUPS)
             return n == GRAM_BIN and g in GRAM_GROUPS
 
+        def is_scalar(group):
+            n, g = divmod(group, GROUPS)
+            return n != GRAM_BIN and g in SCALAR_GROUPS
+
         def features_of(group, t, j):
             u, e = divmod(t, PAIR)
             return loaded_of[group][:].rearrange("p (j u q e) -> p j u e q", j=GROUP, u=HALVES, e=PAIR)[:, j, u, e, :]
@@ -177,7 +183,7 @@ def tile_gmpahead_pb_t_kernel(tc, emb, gamma, beta, fc1d, out):
         def summed_part(n):
             if n == GRAM_BIN:
                 return range(PACK), [(n * GROUPS + g, j) for g in GRAM_GROUPS for j in range(GROUP)]
-            return range(PACK - PAIR, PACK), [(n * GROUPS + g, j) for g in range(GROUPS) for j in range(GROUP // CHUNKS, GROUP)]
+            return range(PACK - PAIR, PACK), [(n * GROUPS + g, j) for g in SCALAR_GROUPS for j in range(GROUP // CHUNKS, GROUP)]
 
         def gram_stage(group):
             if group % GROUPS == GRAM_GROUPS[0]:
@@ -201,13 +207,14 @@ def tile_gmpahead_pb_t_kernel(tc, emb, gamma, beta, fc1d, out):
 
         def scalar_squares_stage(group):
             n, g = divmod(group, GROUPS)
-            if g == 0:
-                parts = per_bin.tile([P, PAIR, GROUPS], F32)
+            k = SCALAR_GROUPS.index(g)
+            if k == 0:
+                parts = per_bin.tile([P, PAIR, len(SCALAR_GROUPS)], F32)
                 parts_of[n] = parts
             chunk = turned_of[group][:, HALVES * COLS - BN_CHUNK // PAIR :].bitcast(BF16).rearrange("p (c e) -> p e c", e=PAIR)
             for e in range(PAIR):
                 junk = scrap.tile([P, BN_CHUNK // PAIR], BF16)
-                nc.scalar.activation(out=junk[:], in_=chunk[:, e, :], func=ACT.Square, accum_out=parts_of[n][:, e, g : g + 1])
+                nc.scalar.activation(out=junk[:], in_=chunk[:, e, :], func=ACT.Square, accum_out=parts_of[n][:, e, k : k + 1])
 
         def sums_stage(n):
             rows, tiles = summed_part(n)
@@ -244,7 +251,7 @@ def tile_gmpahead_pb_t_kernel(tc, emb, gamma, beta, fc1d, out):
                 first_slot_of[n] = [GROUPS * CHUNKS] * HALVES
             values = turned_of[group][:, u * COLS : (u + 1) * COLS].bitcast(BF16)
             for h in range(CHUNKS):
-                if n != GRAM_BIN and (u, h) == (HALVES - 1, CHUNKS - 1):
+                if is_scalar(group) and (u, h) == (HALVES - 1, CHUNKS - 1):
                     continue
                 first_slot_of[n][u] -= 1
                 nc.vector.bn_stats(out=stats_of[n][:, u, first_slot_of[n][u], :], in_=values[:, h * BN_CHUNK : (h + 1) * BN_CHUNK])
@@ -273,13 +280,15 @@ def tile_gmpahead_pb_t_kernel(tc, emb, gamma, beta, fc1d, out):
 
         def affine_stage(group):
             gain, shift = coefficients_of[group // GROUPS]
+            gpsimd_rows = PACK if 0 < group and is_group(group + AFFINE_LAG - STATS_LAG) else SHARED_GPSIMD_ROWS
             y_t = columns.tile([P, PACK, COLS], F32)
             columns_of[("samples", group)] = y_t[:]
             for u in range(HALVES):
                 values = turned_of[group][:, u * COLS : (u + 1) * COLS].bitcast(BF16).rearrange("p (c e) -> p c e", e=PAIR)
                 for e in range(PAIR):
                     t = PAIR * u + e
-                    nc.gpsimd.tensor_scalar(
+                    engine = nc.gpsimd if t < gpsimd_rows else nc.vector
+                    engine.tensor_scalar(
                         out=y_t[:, t, :], in0=values[:, :, e], scalar1=gain[:, t : t + 1], scalar2=shift[:, t : t + 1], op0=ALU.mult, op1=ALU.add
                     )
 
@@ -411,7 +420,7 @@ def tile_gmpahead_pb_t_kernel(tc, emb, gamma, beta, fc1d, out):
                 inverse_stage(("samples", square))
             if is_group(product):
                 leave_stage(product, 1)
-            if is_group(step - STATS_LAG) and (step - STATS_LAG) // GROUPS != GRAM_BIN:
+            if is_group(step - STATS_LAG) and is_scalar(step - STATS_LAG):
                 scalar_squares_stage(step - STATS_LAG)
             if is_group(turn):
                 turn_stage(turn)
@@ -425,6 +434,8 @@ def tile_gmpahead_pb_t_kernel(tc, emb, gamma, beta, fc1d, out):
                 squares_stage(key, range(CLASS_TILES))
                 inverse_stage(key)
 
+            if is_group(step - AFFINE_LAG):
+                affine_stage(step - AFFINE_LAG)
             for key in columns_due(step - SCALE_AFTER) + classes_due(step - CLASSES_SCALE_AFTER):
                 scale_stage(key)
             if bn_group:
@@ -434,6 +445,3 @@ def tile_gmpahead_pb_t_kernel(tc, emb, gamma, beta, fc1d, out):
             for n in bin_due(step, MOMENTS_LAG):
                 summed_statistics_stage(n)
                 moments_stage(n)
-
-            if is_group(step - AFFINE_LAG):
-                affine_stage(step - AFFINE_LAG)

@@ -55,7 +55,7 @@ GRAM_GROUPS = (0, 2, 4, 6)
 SCALAR_GROUPS = (1, 2, 3, 5, 6, 7)
 
 SHARED_GPSIMD_ROWS = 2
-RUN = 4
+RUN = 2
 TURN_BANKS = 2
 SCALAR_BANKS = 4
 SPREAD_BANKS = 2

@@ -45,16 +45,18 @@ SQUARES_LAG = AFFINE_LAG + 1
 SCALE_AFTER = 1
 QUANTISE_AFTER = 2
 MATMUL_AFTER = 2
-SMALL_INPUTS_STEP = 2
+SMALL_INPUTS_STEP = 6
+CLASSES_LOAD_STEP = 1
 CLASSES_STEP = 3
 CLASSES_SCALE_AFTER = 2
 LAST_STEP = ALL_GROUPS - 1 + SQUARES_LAG + MATMUL_AFTER
 
 GRAM_BIN = 0
 GRAM_GROUPS = (0, 2, 4, 6)
-SCALAR_GROUPS = (1, 2, 3, 5, 6, 7)
+SCALAR_GROUPS = (1, 3, 5, 7)
 
 SHARED_GPSIMD_ROWS = 2
+COLUMN_BUFS = 4
 RUN = 2
 TURN_BANKS = 2
 SCALAR_BANKS = 4
@@ -70,7 +72,7 @@ def tile_gmpahead_pb_t_kernel(tc, emb, gamma, beta, fc1d, out):
         const = stack.enter_context(tc.tile_pool(name="const", bufs=1))
         loads = stack.enter_context(tc.tile_pool(name="loads", bufs=LOAD_LEAD + GROUPS))
         turned = stack.enter_context(tc.tile_pool(name="turned", bufs=AFFINE_LAG + 2))
-        columns = stack.enter_context(tc.tile_pool(name="columns", bufs=SQUARES_LAG - AFFINE_LAG + SCALE_AFTER + 2))
+        columns = stack.enter_context(tc.tile_pool(name="columns", bufs=COLUMN_BUFS))
         small = stack.enter_context(tc.tile_pool(name="small", bufs=4))
         per_bin = stack.enter_context(tc.tile_pool(name="per_bin", bufs=2))
         scrap = stack.enter_context(tc.tile_pool(name="scrap", bufs=4))
@@ -281,8 +283,10 @@ def tile_gmpahead_pb_t_kernel(tc, emb, gamma, beta, fc1d, out):
         def affine_stage(group):
             gain, shift = coefficients_of[group // GROUPS]
             gpsimd_rows = PACK if 0 < group and is_group(group + AFFINE_LAG - STATS_LAG) else SHARED_GPSIMD_ROWS
-            y_t = columns.tile([P, PACK, COLS], F32)
-            columns_of[("samples", group)] = y_t[:]
+            whole = columns.tile([P, PACK * COLS * 3 // 2], F32, align_bytes=64)
+            y_t = whole[:, 0 : PACK * COLS].rearrange("p (t c) -> p t c", t=PACK)
+            columns_of[("samples", group)] = y_t
+            grouped_of[("samples", group)] = whole[:, PACK * COLS :].bitcast(BF16).rearrange("p (c t) -> p c t", t=PACK)
             for u in range(HALVES):
                 values = turned_of[group][:, u * COLS : (u + 1) * COLS].bitcast(BF16).rearrange("p (c e) -> p c e", e=PAIR)
                 for e in range(PAIR):
@@ -337,10 +341,11 @@ def tile_gmpahead_pb_t_kernel(tc, emb, gamma, beta, fc1d, out):
 
         def scale_stage(key):
             cols = tiles_of(key) * P
-            grouped = quant.tile([P, COLS, PACK], BF16, align_bytes=64)
-            grouped_of[key] = grouped
+            if key not in grouped_of:
+                grouped = quant.tile([P, CLASSES, PACK], BF16, align_bytes=64)
+                grouped_of[key] = grouped[:]
             nc.vector.tensor_tensor(
-                out=grouped[:, 0:cols, :].rearrange("p (c i) t -> p c t i", i=RUN),
+                out=grouped_of[key].rearrange("p (c i) t -> p c t i", i=RUN),
                 in0=columns_of[key].rearrange("p t (c i) -> p c t i", i=RUN),
                 in1=spread_of[key][:, 0:cols].rearrange("p (c i) -> p c i", i=RUN).unsqueeze(2).to_broadcast([P, cols // RUN, PACK, RUN]),
                 op=ALU.mult,
@@ -355,7 +360,7 @@ def tile_gmpahead_pb_t_kernel(tc, emb, gamma, beta, fc1d, out):
             else:
                 operand_of[key] = (fc_codes[:, key[1], :], fc_planes[:, key[1], :])
             nc.vector.quantize_mx(
-                out=operand_of[key][0].bitcast(FP8X4), scales=operand_of[key][1], in_=grouped_of[key][:, 0:cols, :].rearrange("p c t -> p (c t)")
+                out=operand_of[key][0].bitcast(FP8X4), scales=operand_of[key][1], in_=grouped_of[key].rearrange("p c t -> p (c t)")
             )
 
 
@@ -388,10 +393,11 @@ def tile_gmpahead_pb_t_kernel(tc, emb, gamma, beta, fc1d, out):
 
         for group in range(LOAD_LEAD):
             load_stage(group)
-        nc.sync.dma_start(out=fc_raw[:], in_=fc1d.rearrange("n (u p e) k -> p (n u) (e k)", u=HALVES, e=PAIR))
         for step in range(LAST_STEP + 1):
             if is_group(step + LOAD_LEAD):
                 load_stage(step + LOAD_LEAD)
+            if step == CLASSES_LOAD_STEP:
+                nc.sync.dma_start(out=fc_raw[:], in_=fc1d.rearrange("n (u p e) k -> p (n u) (e k)", u=HALVES, e=PAIR))
 
             for n in bin_due(step, COEFFICIENTS_LAG):
                 deviation_stage(n)

@@ -36,6 +36,8 @@ STATS = 6
 FLOPS = 2 * BINS * SAMPLES * FEATURES * CLASSES
 
 LOAD_LEAD = 3
+LOAD_BUFS = 16
+FC_AFTER = 2
 STATS_LAG = 1
 FILL = 1
 MOMENTS_LAG = GROUPS - 1 + STATS_LAG
@@ -46,17 +48,27 @@ SCALE_AFTER = 1
 QUANTISE_AFTER = 2
 MATMUL_AFTER = 2
 SMALL_INPUTS_STEP = 6
-CLASSES_LOAD_STEP = 1
 CLASSES_STEP = 3
+CLASSES_EVERY = 1
+CLASSES_SCALE_STEP = 11
+CPS = 2
+LOAD_ORDER = (0, 1, 2, 3, 8, 4, 9, 5, 10, 6, 11, 7, 12)
 CLASSES_SCALE_AFTER = 2
-LAST_STEP = ALL_GROUPS - 1 + SQUARES_LAG + MATMUL_AFTER
+LAST_GROUP = ALL_GROUPS - 1
+LAST_STEP = LAST_GROUP + SQUARES_LAG + SCALE_AFTER
 
-GRAM_BIN = 0
-GRAM_GROUPS = (0, 2, 4, 6)
+GRAM_BIN = 1
+GRAM_GROUPS = (0, 1, 2, 3, 4)
+GRAM_LEAD = 5
 SCALAR_GROUPS = (1, 3, 5, 7)
+FIRST_SCALAR_GROUPS = ()
 
 SHARED_GPSIMD_ROWS = 2
+R0 = 0
+NEARLY = 1
+RN = 2
 COLUMN_BUFS = 4
+GRAM_END = GRAM_BIN * GROUPS + GRAM_GROUPS[-1] - GRAM_LEAD + STATS_LAG
 RUN = 2
 TURN_BANKS = 2
 SCALAR_BANKS = 4
@@ -70,7 +82,7 @@ def tile_gmpahead_pb_t_kernel(tc, emb, gamma, beta, fc1d, out):
 
     with ExitStack() as stack:
         const = stack.enter_context(tc.tile_pool(name="const", bufs=1))
-        loads = stack.enter_context(tc.tile_pool(name="loads", bufs=LOAD_LEAD + GROUPS))
+        loads = stack.enter_context(tc.tile_pool(name="loads", bufs=LOAD_BUFS))
         turned = stack.enter_context(tc.tile_pool(name="turned", bufs=AFFINE_LAG + 2))
         columns = stack.enter_context(tc.tile_pool(name="columns", bufs=COLUMN_BUFS))
         small = stack.enter_context(tc.tile_pool(name="small", bufs=4))
@@ -140,8 +152,12 @@ def tile_gmpahead_pb_t_kernel(tc, emb, gamma, beta, fc1d, out):
             return keys
 
         def classes_due(step):
-            n, rest = divmod(step - CLASSES_STEP, 2)
+            n, rest = divmod(step - CLASSES_STEP, CLASSES_EVERY)
             return [("classes", n)] if rest == 0 and is_bin(n) else []
+
+        def classes_scaled(step):
+            first = (step - CLASSES_SCALE_STEP) * CPS
+            return [("classes", n) for n in range(first, first + CPS) if is_bin(n)]
 
         def tiles_of(key):
             return GROUP if key[0] == "samples" else CLASS_TILES
@@ -174,9 +190,12 @@ def tile_gmpahead_pb_t_kernel(tc, emb, gamma, beta, fc1d, out):
             n, g = divmod(group, GROUPS)
             return n == GRAM_BIN and g in GRAM_GROUPS
 
+        def scalar_groups(n):
+            return FIRST_SCALAR_GROUPS if n == 0 else SCALAR_GROUPS
+
         def is_scalar(group):
             n, g = divmod(group, GROUPS)
-            return n != GRAM_BIN and g in SCALAR_GROUPS
+            return n != GRAM_BIN and g in scalar_groups(n)
 
         def features_of(group, t, j):
             u, e = divmod(t, PAIR)
@@ -185,7 +204,9 @@ def tile_gmpahead_pb_t_kernel(tc, emb, gamma, beta, fc1d, out):
         def summed_part(n):
             if n == GRAM_BIN:
                 return range(PACK), [(n * GROUPS + g, j) for g in GRAM_GROUPS for j in range(GROUP)]
-            return range(PACK - PAIR, PACK), [(n * GROUPS + g, j) for g in SCALAR_GROUPS for j in range(GROUP // CHUNKS, GROUP)]
+            if not scalar_groups(n):
+                return range(0), []
+            return range(PACK - PAIR, PACK), [(n * GROUPS + g, j) for g in scalar_groups(n) for j in range(GROUP // CHUNKS, GROUP)]
 
         def gram_stage(group):
             if group % GROUPS == GRAM_GROUPS[0]:
@@ -209,9 +230,9 @@ def tile_gmpahead_pb_t_kernel(tc, emb, gamma, beta, fc1d, out):
 
         def scalar_squares_stage(group):
             n, g = divmod(group, GROUPS)
-            k = SCALAR_GROUPS.index(g)
+            k = scalar_groups(n).index(g)
             if k == 0:
-                parts = per_bin.tile([P, PAIR, len(SCALAR_GROUPS)], F32)
+                parts = per_bin.tile([P, PAIR, len(scalar_groups(n))], F32)
                 parts_of[n] = parts
             chunk = turned_of[group][:, HALVES * COLS - BN_CHUNK // PAIR :].bitcast(BF16).rearrange("p (c e) -> p e c", e=PAIR)
             for e in range(PAIR):
@@ -228,6 +249,13 @@ def tile_gmpahead_pb_t_kernel(tc, emb, gamma, beta, fc1d, out):
                         out=spread[:, t : t + 1], lhsT=features_of(group, t, j), rhs=ones[:], start=(group, j) == tiles[0], stop=(group, j) == tiles[-1]
                     )
 
+        def stats_tile(n):
+            if n not in stats_of:
+                stats = per_bin.tile([P, HALVES, GROUPS * CHUNKS + 1, STATS], F32)
+                stats_of[n] = stats
+                first_slot_of[n] = [GROUPS * CHUNKS] * HALVES
+            return stats_of[n]
+
         def summed_statistics_stage(n):
             rows, tiles = summed_part(n)
             samples = len(tiles) * P
@@ -238,7 +266,7 @@ def tile_gmpahead_pb_t_kernel(tc, emb, gamma, beta, fc1d, out):
                 nc.vector.reduce_sum(out=squares[:], in_=parts_of[n][:], axis=mybir.AxisListType.X)
             pairs = "p (u e) -> p u e"
             sums = sums_of[n].rearrange(pairs, e=PAIR)
-            slots = stats_of[n][:, first:, GROUPS * CHUNKS, :].rearrange("p u (e s) -> p u e s", e=PAIR)
+            slots = stats_tile(n)[:, first:, GROUPS * CHUNKS, :].rearrange("p u (e s) -> p u e s", e=PAIR)
             nc.vector.memset(slots[:, :, :, 0], float(samples))
             nc.vector.tensor_scalar_mul(out=slots[:, :, :, 1], in0=sums, scalar1=1.0 / samples)
             sum_mean = per_bin.tile([P, HALVES, PAIR], F32)
@@ -247,16 +275,13 @@ def tile_gmpahead_pb_t_kernel(tc, emb, gamma, beta, fc1d, out):
 
         def statistics_stage(group, u):
             n = group // GROUPS
-            if n not in stats_of:
-                stats = per_bin.tile([P, HALVES, GROUPS * CHUNKS + 1, STATS], F32)
-                stats_of[n] = stats
-                first_slot_of[n] = [GROUPS * CHUNKS] * HALVES
+            stats = stats_tile(n)
             values = turned_of[group][:, u * COLS : (u + 1) * COLS].bitcast(BF16)
             for h in range(CHUNKS):
                 if is_scalar(group) and (u, h) == (HALVES - 1, CHUNKS - 1):
                     continue
                 first_slot_of[n][u] -= 1
-                nc.vector.bn_stats(out=stats_of[n][:, u, first_slot_of[n][u], :], in_=values[:, h * BN_CHUNK : (h + 1) * BN_CHUNK])
+                nc.vector.bn_stats(out=stats[:, u, first_slot_of[n][u], :], in_=values[:, h * BN_CHUNK : (h + 1) * BN_CHUNK])
 
         def moments_stage(n):
             moments = per_bin.tile([P, PACK, 2], F32)
@@ -280,9 +305,16 @@ def tile_gmpahead_pb_t_kernel(tc, emb, gamma, beta, fc1d, out):
             nc.vector.tensor_sub(out=shift[:], in0=gb_t[:, BINS + n, :], in1=gain_mean[:])
             coefficients_of[n] = (gain, shift)
 
+        def gpsimd_rows_of(group):
+            if group == 0:
+                return R0
+            if group < NEARLY:
+                return RN
+            return PACK if is_group(group + AFFINE_LAG - STATS_LAG) else SHARED_GPSIMD_ROWS
+
         def affine_stage(group):
             gain, shift = coefficients_of[group // GROUPS]
-            gpsimd_rows = PACK if 0 < group and is_group(group + AFFINE_LAG - STATS_LAG) else SHARED_GPSIMD_ROWS
+            gpsimd_rows = gpsimd_rows_of(group)
             whole = columns.tile([P, PACK * COLS * 3 // 2], F32, align_bytes=64)
             y_t = whole[:, 0 : PACK * COLS].rearrange("p (t c) -> p t c", t=PACK)
             columns_of[("samples", group)] = y_t
@@ -339,71 +371,80 @@ def tile_gmpahead_pb_t_kernel(tc, emb, gamma, beta, fc1d, out):
             for j in range(tiles_of(key)):
                 nc.tensor.transpose(out=spread[:, j * P : (j + 1) * P], in_=inverse_of[key][:, j : j + 1].to_broadcast([P, P]), identity=ident[:])
 
-        def scale_stage(key):
+        def columns_of_half(key, half):
             cols = tiles_of(key) * P
+            return slice(0, cols) if half is None else slice(half * cols // 2, (half + 1) * cols // 2)
+
+        def scale_stage(key, half=None):
+            cols = columns_of_half(key, half)
+            count = cols.stop - cols.start
             if key not in grouped_of:
                 grouped = quant.tile([P, CLASSES, PACK], BF16, align_bytes=64)
                 grouped_of[key] = grouped[:]
             nc.vector.tensor_tensor(
-                out=grouped_of[key].rearrange("p (c i) t -> p c t i", i=RUN),
-                in0=columns_of[key].rearrange("p t (c i) -> p c t i", i=RUN),
-                in1=spread_of[key][:, 0:cols].rearrange("p (c i) -> p c i", i=RUN).unsqueeze(2).to_broadcast([P, cols // RUN, PACK, RUN]),
+                out=grouped_of[key][:, cols, :].rearrange("p (c i) t -> p c t i", i=RUN),
+                in0=columns_of[key][:, :, cols].rearrange("p t (c i) -> p c t i", i=RUN),
+                in1=spread_of[key][:, cols].rearrange("p (c i) -> p c i", i=RUN).unsqueeze(2).to_broadcast([P, count // RUN, PACK, RUN]),
                 op=ALU.mult,
             )
 
-        def quantise_stage(key):
-            cols = tiles_of(key) * P
-            if key[0] == "samples":
-                codes = quant.tile([P, COLS], U32, align_bytes=64)
-                plane = quant.tile([P, COLS], U8, align_bytes=64)
-                operand_of[key] = (codes[:], plane[:])
-            else:
-                operand_of[key] = (fc_codes[:, key[1], :], fc_planes[:, key[1], :])
+        def quantise_stage(key, half=None):
+            cols = columns_of_half(key, half)
+            if key not in operand_of:
+                if key[0] == "samples":
+                    codes = quant.tile([P, COLS], U32, align_bytes=64)
+                    plane = quant.tile([P, COLS], U8, align_bytes=64)
+                    operand_of[key] = (codes[:], plane[:])
+                else:
+                    operand_of[key] = (fc_codes[:, key[1], :], fc_planes[:, key[1], :])
+            codes, plane = operand_of[key]
             nc.vector.quantize_mx(
-                out=operand_of[key][0].bitcast(FP8X4), scales=operand_of[key][1], in_=grouped_of[key].rearrange("p c t -> p (c t)")
+                out=codes[:, cols].bitcast(FP8X4), scales=plane[:, cols], in_=grouped_of[key][:, cols, :].rearrange("p c t -> p (c t)")
             )
 
 
-        def matmul_stage(group):
+        def matmul_stage(group, half):
             codes, plane = operand_of[("samples", group)]
             class_codes, class_plane = operand_of[("classes", group // GROUPS)]
-            product_of[group] = []
-            for first in range(0, GROUP, BANK_TILES):
-                acc = psum_scalar.tile([P, BANK_TILES, CLASSES], F32, tag="bank")
-                product_of[group].append(acc)
-                for i in range(BANK_TILES):
-                    samples = slice((first + i) * P, (first + i + 1) * P)
-                    nc.tensor.matmul_mx(
-                        out=acc[:, i, :],
-                        lhsT=codes[:, samples].bitcast(FP8X4),
-                        lhsT_scale=plane[:, samples],
-                        rhs=class_codes.bitcast(FP8X4),
-                        rhs_scale=class_plane,
-                        start=True,
-                        stop=True,
-                    )
-            logits = results.tile([P, GROUP, CLASSES], F32)
-            logits_of[group] = logits
+            acc = psum_scalar.tile([P, BANK_TILES, CLASSES], F32, tag="bank")
+            product_of[group, half] = acc
+            for i in range(BANK_TILES):
+                samples = slice((half * BANK_TILES + i) * P, (half * BANK_TILES + i + 1) * P)
+                nc.tensor.matmul_mx(
+                    out=acc[:, i, :],
+                    lhsT=codes[:, samples].bitcast(FP8X4),
+                    lhsT_scale=plane[:, samples],
+                    rhs=class_codes.bitcast(FP8X4),
+                    rhs_scale=class_plane,
+                    start=True,
+                    stop=True,
+                )
 
         def leave_stage(group, half):
-            n, g = divmod(group, GROUPS)
-            nc.scalar.copy(out=logits_of[group][:, half * BANK_TILES : (half + 1) * BANK_TILES, :], in_=product_of[group][half][:])
-            if half == GROUP // BANK_TILES - 1:
-                nc.sync.dma_start(out=out_tiles[:, g * GROUP : (g + 1) * GROUP, n, :], in_=logits_of[group][:])
+            if half == 0:
+                logits = results.tile([P, GROUP, CLASSES], F32)
+                logits_of[group] = logits
+            nc.scalar.copy(out=logits_of[group][:, half * BANK_TILES : (half + 1) * BANK_TILES, :], in_=product_of[group, half][:])
 
-        for group in range(LOAD_LEAD):
+        def store_stage(group, tiles):
+            n, g = divmod(group, GROUPS)
+            nc.sync.dma_start(out=out_tiles[:, g * GROUP + tiles.start : g * GROUP + tiles.stop, n, :], in_=logits_of[group][:, tiles, :])
+
+        order = LOAD_ORDER
+        for group in order:
             load_stage(group)
-        for step in range(LAST_STEP + 1):
-            if is_group(step + LOAD_LEAD):
-                load_stage(step + LOAD_LEAD)
-            if step == CLASSES_LOAD_STEP:
+            if group == FC_AFTER:
                 nc.sync.dma_start(out=fc_raw[:], in_=fc1d.rearrange("n (u p e) k -> p (n u) (e k)", u=HALVES, e=PAIR))
+        for step in range(LAST_STEP + 1):
+            if is_group(step + LOAD_LEAD) and step + LOAD_LEAD not in order:
+                load_stage(step + LOAD_LEAD)
 
             for n in bin_due(step, COEFFICIENTS_LAG):
                 deviation_stage(n)
 
-            for key in columns_due(step - QUANTISE_AFTER) + classes_due(step - CLASSES_SCALE_AFTER - 1):
-                quantise_stage(key)
+            for key in columns_due(step - QUANTISE_AFTER) + classes_scaled(step - 1):
+                if key not in operand_of:
+                    quantise_stage(key)
             if step == SMALL_INPUTS_STEP + 1:
                 keep_gamma_and_beta()
             bn_group = is_group(step - STATS_LAG) and not is_gram(step - STATS_LAG)
@@ -411,43 +452,60 @@ def tile_gmpahead_pb_t_kernel(tc, emb, gamma, beta, fc1d, out):
                 statistics_stage(step - STATS_LAG, 0)
             for n in bin_due(step, COEFFICIENTS_LAG):
                 coefficients_stage(n)
+                if n == 0:
+                    affine_stage(0)
 
             turn, square, product = step, step - SQUARES_LAG, step - SQUARES_LAG - MATMUL_AFTER
             if is_group(square):
                 squares_stage(("samples", square), range(0, GROUP // 2))
-            for key in columns_due(step - SCALE_AFTER) + classes_due(step - CLASSES_SCALE_AFTER):
+            for key in columns_due(step - SCALE_AFTER) + classes_scaled(step):
                 spread_stage(key)
             if is_group(square):
                 squares_stage(("samples", square), range(GROUP // 2, GROUP))
-            if is_group(product):
-                matmul_stage(product)
+            if is_group(product) and product != LAST_GROUP:
+                matmul_stage(product, 0)
+                matmul_stage(product, 1)
                 leave_stage(product, 0)
             if is_group(square):
                 inverse_stage(("samples", square))
-            if is_group(product):
+            if is_group(product) and product != LAST_GROUP:
                 leave_stage(product, 1)
+                store_stage(product, slice(0, GROUP))
             if is_group(step - STATS_LAG) and is_scalar(step - STATS_LAG):
                 scalar_squares_stage(step - STATS_LAG)
             if is_group(turn):
                 turn_stage(turn)
-                if is_gram(turn):
-                    gram_stage(turn)
+            if is_group(turn + GRAM_LEAD) and is_gram(turn + GRAM_LEAD):
+                gram_stage(turn + GRAM_LEAD)
             for n in bin_due(step, GROUPS - 1):
-                sums_stage(n)
+                if n != GRAM_BIN and scalar_groups(n):
+                    sums_stage(n)
+            if step == GRAM_END:
+                sums_stage(GRAM_BIN)
             if step == SMALL_INPUTS_STEP:
                 turn_gamma_and_beta()
             for key in classes_due(step):
                 squares_stage(key, range(CLASS_TILES))
                 inverse_stage(key)
 
-            if is_group(step - AFFINE_LAG):
+            if is_group(step - AFFINE_LAG) and step > AFFINE_LAG:
                 affine_stage(step - AFFINE_LAG)
-            for key in columns_due(step - SCALE_AFTER) + classes_due(step - CLASSES_SCALE_AFTER):
-                scale_stage(key)
+            for key in columns_due(step - SCALE_AFTER) + classes_scaled(step):
+                if key == ("samples", LAST_GROUP):
+                    for half in range(GROUP // BANK_TILES):
+                        scale_stage(key, half)
+                        quantise_stage(key, half)
+                        matmul_stage(LAST_GROUP, half)
+                        leave_stage(LAST_GROUP, half)
+                        store_stage(LAST_GROUP, slice(half * BANK_TILES, (half + 1) * BANK_TILES))
+                else:
+                    scale_stage(key)
             if bn_group:
                 statistics_stage(step - STATS_LAG, 1)
-            if step == GRAM_BIN * GROUPS + GRAM_GROUPS[-1] + STATS_LAG:
+            if step == GRAM_END + 1:
                 gram_squares_stage()
+                summed_statistics_stage(GRAM_BIN)
             for n in bin_due(step, MOMENTS_LAG):
-                summed_statistics_stage(n)
+                if n != GRAM_BIN and scalar_groups(n):
+                    summed_statistics_stage(n)
                 moments_stage(n)

@@ -256,24 +256,26 @@ def tile_gmpahead_pb_t_kernel(tc, emb, gamma, beta, fc1d, out):
                 first_slot_of[n] = [GROUPS * CHUNKS] * HALVES
             return stats_of[n]
 
-        def summed_statistics_stage(n):
+        def summed_statistics_stage(n, between):
             rows, tiles = summed_part(n)
             samples = len(tiles) * P
             first = rows[0] // PAIR
+            pairs = "p (u e) -> p u e"
+            sums = sums_of[n].rearrange(pairs, e=PAIR)
+            slots = stats_tile(n)[:, first:, GROUPS * CHUNKS, :].rearrange("p u (e s) -> p u e s", e=PAIR)
+            nc.vector.tensor_scalar_mul(out=slots[:, :, :, 1], in0=sums, scalar1=1.0 / samples)
             if n != GRAM_BIN:
                 squares = per_bin.tile([P, PAIR], F32)
                 squares_of[n] = squares[:]
                 nc.vector.reduce_sum(out=squares[:], in_=parts_of[n][:], axis=mybir.AxisListType.X)
-            pairs = "p (u e) -> p u e"
-            sums = sums_of[n].rearrange(pairs, e=PAIR)
-            slots = stats_tile(n)[:, first:, GROUPS * CHUNKS, :].rearrange("p u (e s) -> p u e s", e=PAIR)
-            nc.vector.memset(slots[:, :, :, 0], float(samples))
-            nc.vector.tensor_scalar_mul(out=slots[:, :, :, 1], in0=sums, scalar1=1.0 / samples)
+            between[0]()
             sum_mean = per_bin.tile([P, HALVES, PAIR], F32)
             nc.vector.tensor_mul(out=sum_mean[:, first:, :], in0=sums, in1=slots[:, :, :, 1])
+            between[1]()
             nc.vector.tensor_sub(out=slots[:, :, :, 2], in0=squares_of[n].rearrange(pairs, e=PAIR), in1=sum_mean[:, first:, :])
+            nc.vector.memset(slots[:, :, :, 0], float(samples))
 
-        def statistics_stage(group, u):
+        def statistics_stage(group, u, between=()):
             n = group // GROUPS
             stats = stats_tile(n)
             values = turned_of[group][:, u * COLS : (u + 1) * COLS].bitcast(BF16)
@@ -282,14 +284,24 @@ def tile_gmpahead_pb_t_kernel(tc, emb, gamma, beta, fc1d, out):
                     continue
                 first_slot_of[n][u] -= 1
                 nc.vector.bn_stats(out=stats[:, u, first_slot_of[n][u], :], in_=values[:, h * BN_CHUNK : (h + 1) * BN_CHUNK])
+                if between:
+                    between[h]()
 
         def moments_stage(n):
             moments = per_bin.tile([P, PACK, 2], F32)
-            for u in range(HALVES):
-                last = GROUPS * CHUNKS + (PAIR * u in summed_part(n)[0])
-                for e in range(PAIR):
-                    nc.vector.bn_aggr(out=moments[:, PAIR * u + e, :], in_=stats_of[n][:, u, first_slot_of[n][u] : last, 3 * e : 3 * e + 3])
             moments_of[n] = moments
+
+            def row_moments(t):
+                u, e = divmod(t, PAIR)
+                last = GROUPS * CHUNKS + (t in summed_part(n)[0])
+                nc.vector.bn_aggr(out=moments[:, t, :], in_=stats_of[n][:, u, first_slot_of[n][u] : last, 3 * e : 3 * e + 3])
+
+            rows = list(range(PACK))
+            if n != GRAM_BIN and scalar_groups(n):
+                summed_statistics_stage(n, [lambda: row_moments(0), lambda: row_moments(1)])
+                rows = rows[PAIR:]
+            for t in rows:
+                row_moments(t)
 
         def deviation_stage(n):
             rstd = per_bin.tile([P, PACK], F32)
@@ -298,12 +310,14 @@ def tile_gmpahead_pb_t_kernel(tc, emb, gamma, beta, fc1d, out):
 
         def coefficients_stage(n):
             gain = per_bin.tile([P, PACK], F32)
-            nc.vector.tensor_mul(out=gain[:], in0=gb_t[:, n, :], in1=deviation_of[n][:])
             gain_mean = per_bin.tile([P, PACK], F32)
-            nc.vector.tensor_mul(out=gain_mean[:], in0=gain[:], in1=moments_of[n][:, :, 0])
             shift = per_bin.tile([P, PACK], F32)
-            nc.vector.tensor_sub(out=shift[:], in0=gb_t[:, BINS + n, :], in1=gain_mean[:])
             coefficients_of[n] = (gain, shift)
+            return [
+                lambda: nc.vector.tensor_mul(out=gain[:], in0=gb_t[:, n, :], in1=deviation_of[n][:]),
+                lambda: nc.vector.tensor_mul(out=gain_mean[:], in0=gain[:], in1=moments_of[n][:, :, 0]),
+                lambda: nc.vector.tensor_sub(out=shift[:], in0=gb_t[:, BINS + n, :], in1=gain_mean[:]),
+            ]
 
         def gpsimd_rows_of(group):
             if group == 0:
@@ -448,12 +462,16 @@ def tile_gmpahead_pb_t_kernel(tc, emb, gamma, beta, fc1d, out):
             if step == SMALL_INPUTS_STEP + 1:
                 keep_gamma_and_beta()
             bn_group = is_group(step - STATS_LAG) and not is_gram(step - STATS_LAG)
+            coefficients = [part for n in bin_due(step, COEFFICIENTS_LAG) for part in coefficients_stage(n)]
+            if coefficients:
+                coefficients[0]()
             if bn_group:
-                statistics_stage(step - STATS_LAG, 0)
-            for n in bin_due(step, COEFFICIENTS_LAG):
-                coefficients_stage(n)
-                if n == 0:
-                    affine_stage(0)
+                statistics_stage(step - STATS_LAG, 0, coefficients[1:])
+            elif coefficients:
+                coefficients[1]()
+                coefficients[2]()
+            if step == COEFFICIENTS_LAG:
+                affine_stage(0)
 
             turn, square, product = step, step - SQUARES_LAG, step - SQUARES_LAG - MATMUL_AFTER
             if is_group(square):
@@ -503,9 +521,6 @@ def tile_gmpahead_pb_t_kernel(tc, emb, gamma, beta, fc1d, out):
             if bn_group:
                 statistics_stage(step - STATS_LAG, 1)
             if step == GRAM_END + 1:
-                gram_squares_stage()
-                summed_statistics_stage(GRAM_BIN)
+                summed_statistics_stage(GRAM_BIN, [gram_squares_stage, lambda: None])
             for n in bin_due(step, MOMENTS_LAG):
-                if n != GRAM_BIN and scalar_groups(n):
-                    summed_statistics_stage(n)
                 moments_stage(n)

@@ -52,13 +52,13 @@ CLASSES_STEP = 3
 CLASSES_EVERY = 1
 CLASSES_SCALE_STEP = 11
 CPS = 2
-LOAD_ORDER = (0, 1, 2, 3, 8, 4, 9, 5, 10, 6, 11, 7, 12)
+LOAD_ORDER = (0, 1, 2, 3, 8, 4, 9, 5, 10, 6, 11, 7, 12, 13)
 CLASSES_SCALE_AFTER = 2
 LAST_GROUP = ALL_GROUPS - 1
 LAST_STEP = LAST_GROUP + SQUARES_LAG + SCALE_AFTER
 
 GRAM_BIN = 1
-GRAM_GROUPS = (0, 1, 2, 3, 4)
+GRAM_GROUPS = (0, 1, 2, 3, 4, 5)
 GRAM_LEAD = 5
 SCALAR_GROUPS = (1, 3, 5, 7)
 FIRST_SCALAR_GROUPS = ()

@@ -43,7 +43,7 @@ FILL = 1
 MOMENTS_LAG = GROUPS - 1 + STATS_LAG
 COEFFICIENTS_LAG = MOMENTS_LAG + 1
 AFFINE_LAG = COEFFICIENTS_LAG + FILL
-SQUARES_LAG = AFFINE_LAG + 1
+SQUARES_LAG = AFFINE_LAG + 2
 SCALE_AFTER = 1
 QUANTISE_AFTER = 2
 MATMUL_AFTER = 2
@@ -63,7 +63,7 @@ GRAM_LEAD = 5
 SCALAR_GROUPS = (1, 3, 5, 7)
 FIRST_SCALAR_GROUPS = ()
 
-SHARED_GPSIMD_ROWS = 2
+SHARED_GPSIMD_ROWS = 3
 R0 = 0
 NEARLY = 1
 RN = 2

from contextlib import ExitStack

import concourse.mybir as mybir
from concourse.masks import make_identity

F32 = mybir.dt.float32
BF16 = mybir.dt.bfloat16
U32 = mybir.dt.uint32
U8 = mybir.dt.uint8
FP8X4 = mybir.dt.float8_e4m3fn_x4
ALU = mybir.AluOpType
ACT = mybir.ActivationFunctionType

BINS = 4
SAMPLES = 4096
FEATURES = 512
CLASSES = 256
BN_EPS = 1e-5
L2_EPS = 1e-12

P = 128
PACK = 4
HALVES = 2
PAIR = 2
TILES = SAMPLES // P
GROUP = 4
GROUPS = TILES // GROUP
ALL_GROUPS = BINS * GROUPS
COLS = GROUP * P
CLASS_TILES = CLASSES // P
BN_CHUNK = 512
CHUNKS = COLS * PAIR // BN_CHUNK
BANK_TILES = 2
STATS = 6

FLOPS = 2 * BINS * SAMPLES * FEATURES * CLASSES

LOAD_LEAD = 3
LOAD_BUFS = 16
FC_AFTER = 2
STATS_LAG = 1
FILL = 1
MOMENTS_LAG = GROUPS - 1 + STATS_LAG
COEFFICIENTS_LAG = MOMENTS_LAG + 1
AFFINE_LAG = COEFFICIENTS_LAG + FILL
SQUARES_LAG = AFFINE_LAG + 2
SCALE_AFTER = 1
QUANTISE_AFTER = 2
MATMUL_AFTER = 2
SMALL_INPUTS_STEP = 6
CLASSES_STEP = 3
CLASSES_EVERY = 1
CLASSES_SCALE_STEP = 11
CPS = 2
LOAD_ORDER = (0, 1, 2, 3, 8, 4, 9, 5, 10, 6, 11, 7, 12, 13)
CLASSES_SCALE_AFTER = 2
LAST_GROUP = ALL_GROUPS - 1
LAST_STEP = LAST_GROUP + SQUARES_LAG + SCALE_AFTER

GRAM_BIN = 1
GRAM_GROUPS = (0, 1, 2, 3, 4, 5)
GRAM_LEAD = 5
SCALAR_GROUPS = (1, 3, 5, 7)
FIRST_SCALAR_GROUPS = ()

SHARED_GPSIMD_ROWS = 3
R0 = 0
NEARLY = 1
RN = 2
COLUMN_BUFS = 4
GRAM_END = GRAM_BIN * GROUPS + GRAM_GROUPS[-1] - GRAM_LEAD + STATS_LAG
RUN = 2
TURN_BANKS = 2
SCALAR_BANKS = 4
SPREAD_BANKS = 2


def tile_gmpahead_pb_t_kernel(tc, emb, gamma, beta, fc1d, out):
    nc = tc.nc
    emb_tiles = emb.rearrange("n (p j) o -> n p j o", j=TILES)
    out_tiles = out.rearrange("(p j) n k -> p j n k", j=TILES)

    with ExitStack() as stack:
        const = stack.enter_context(tc.tile_pool(name="const", bufs=1))
        loads = stack.enter_context(tc.tile_pool(name="loads", bufs=LOAD_BUFS))
        turned = stack.enter_context(tc.tile_pool(name="turned", bufs=AFFINE_LAG + 2))
        columns = stack.enter_context(tc.tile_pool(name="columns", bufs=COLUMN_BUFS))
        small = stack.enter_context(tc.tile_pool(name="small", bufs=4))
        per_bin = stack.enter_context(tc.tile_pool(name="per_bin", bufs=2))
        scrap = stack.enter_context(tc.tile_pool(name="scrap", bufs=4))
        quant = stack.enter_context(tc.tile_pool(name="quant", bufs=3))
        results = stack.enter_context(tc.tile_pool(name="results", bufs=4))
        psum_turn = stack.enter_context(tc.psum_pool(name="psum_turn", bufs=TURN_BANKS))
        psum_scalar = stack.enter_context(tc.psum_pool(name="psum_scalar", bufs=SCALAR_BANKS))
        psum_spread = stack.enter_context(tc.psum_pool(name="psum_spread", bufs=SPREAD_BANKS))
        stack.enter_context(tc.manual_schedule())

        ident = const.tile([P, P], F32)
        make_identity(nc, ident[:])
        ident_bf = const.tile([P, P], BF16)
        make_identity(nc, ident_bf[:])

        ones = const.tile([P, 1], BF16)
        nc.vector.memset(ones[:], 1.0)

        gb_rows = const.tile([P, HALVES * P], F32)
        nc.vector.memset(gb_rows[:], 0.0)
        nc.scalar.dma_start(out=gb_rows[0:BINS, :].bitcast(BF16), in_=gamma)
        nc.scalar.dma_start(out=gb_rows[BINS : 2 * BINS, :].bitcast(BF16), in_=beta)
        gb_t = const.tile([P, 2 * BINS, PACK], F32)
        fc_raw = const.tile([P, BINS * HALVES, PAIR * CLASSES], BF16)
        fc_codes = const.tile([P, BINS, CLASSES], U32, align_bytes=64)
        fc_planes = const.tile([P, BINS, CLASSES], U8, align_bytes=64)

        loaded_of = {}
        turned_of = {}
        stats_of = {}
        first_slot_of = {}
        moments_of = {}
        deviation_of = {}
        coefficients_of = {}
        product_of = {}
        logits_of = {}
        gram_banks = []
        parts_of = {}
        squares_of = {}
        sums_of = {}
        gb_bank = {}
        columns_of = {}
        for n in range(BINS):
            columns_of[("classes", n)] = fc_raw[:, n * HALVES : (n + 1) * HALVES, :].rearrange("p u (e k) -> p (u e) k", e=PAIR)
        norm_sq_of = {}
        inverse_of = {}
        spread_of = {}
        grouped_of = {}
        operand_of = {}

        def is_group(group):
            return 0 <= group < ALL_GROUPS

        def is_bin(n):
            return 0 <= n < BINS

        def bin_due(step, lag):
            n, rest = divmod(step - lag, GROUPS)
            return [n] if rest == 0 and is_bin(n) else []

        def columns_due(step):
            keys = []
            if is_group(step - SQUARES_LAG):
                keys.append(("samples", step - SQUARES_LAG))
            return keys

        def classes_due(step):
            n, rest = divmod(step - CLASSES_STEP, CLASSES_EVERY)
            return [("classes", n)] if rest == 0 and is_bin(n) else []

        def classes_scaled(step):
            first = (step - CLASSES_SCALE_STEP) * CPS
            return [("classes", n) for n in range(first, first + CPS) if is_bin(n)]

        def tiles_of(key):
            return GROUP if key[0] == "samples" else CLASS_TILES


        def load_stage(group):
            n, g = divmod(group, GROUPS)
            raw = loads.tile([P, GROUP * FEATURES], BF16)
            loaded_of[group] = raw
            pieces = 2 if group == 0 else 1
            tiles = GROUP // pieces
            for piece in range(pieces):
                nc.sync.dma_start(
                    out=raw[:, piece * tiles * FEATURES : (piece + 1) * tiles * FEATURES].rearrange("p (j o) -> p j o", j=tiles),
                    in_=emb_tiles[n, :, g * GROUP + piece * tiles : g * GROUP + (piece + 1) * tiles, :],
                )

        def turn_stage(group):
            words = loaded_of[group][:].bitcast(F32)
            e_t = turned.tile([P, HALVES * COLS], F32)
            turned_of[group] = e_t
            for u in range(HALVES):
                bank = psum_turn.tile([P, COLS], F32, tag="bank")
                for j in range(GROUP):
                    first = (j * HALVES + u) * P
                    nc.tensor.transpose(out=bank[:, j * P : (j + 1) * P], in_=words[:, first : first + P], identity=ident[:])
                nc.scalar.copy(out=e_t[:, u * COLS : (u + 1) * COLS], in_=bank[:])

        def is_gram(group):
            n, g = divmod(group, GROUPS)
            return n == GRAM_BIN and g in GRAM_GROUPS

        def scalar_groups(n):
            return FIRST_SCALAR_GROUPS if n == 0 else SCALAR_GROUPS

        def is_scalar(group):
            n, g = divmod(group, GROUPS)
            return n != GRAM_BIN and g in scalar_groups(n)

        def features_of(group, t, j):
            u, e = divmod(t, PAIR)
            return loaded_of[group][:].rearrange("p (j u q e) -> p j u e q", j=GROUP, u=HALVES, e=PAIR)[:, j, u, e, :]

        def summed_part(n):
            if n == GRAM_BIN:
                return range(PACK), [(n * GROUPS + g, j) for g in GRAM_GROUPS for j in range(GROUP)]
            if not scalar_groups(n):
                return range(0), []
            return range(PACK - PAIR, PACK), [(n * GROUPS + g, j) for g in scalar_groups(n) for j in range(GROUP // CHUNKS, GROUP)]

        def gram_stage(group):
            if group % GROUPS == GRAM_GROUPS[0]:
                for t in range(PACK):
                    bank = psum_scalar.tile([P, P], F32, tag="bank")
                    gram_banks.append(bank)
            for t in range(PACK):
                for j in range(GROUP):
                    some = features_of(group, t, j)
                    tiles = summed_part(GRAM_BIN)[1]
                    nc.tensor.matmul(out=gram_banks[t][:], lhsT=some, rhs=some, start=(group, j) == tiles[0], stop=(group, j) == tiles[-1])

        def gram_squares_stage():
            squares = per_bin.tile([P, PACK], F32)
            squares_of[GRAM_BIN] = squares[:]
            for t in range(PACK):
                diagonal = scrap.tile([P, P], F32)
                nc.vector.scalar_tensor_tensor(
                    out=diagonal[:], in0=gram_banks[t][:], scalar=1.0, in1=ident[:], op0=ALU.mult, op1=ALU.mult, accum_out=squares[:, t : t + 1]
                )

        def scalar_squares_stage(group):
            n, g = divmod(group, GROUPS)
            k = scalar_groups(n).index(g)
            if k == 0:
                parts = per_bin.tile([P, PAIR, len(scalar_groups(n))], F32)
                parts_of[n] = parts
            chunk = turned_of[group][:, HALVES * COLS - BN_CHUNK // PAIR :].bitcast(BF16).rearrange("p (c e) -> p e c", e=PAIR)
            for e in range(PAIR):
                junk = scrap.tile([P, BN_CHUNK // PAIR], BF16)
                nc.scalar.activation(out=junk[:], in_=chunk[:, e, :], func=ACT.Square, accum_out=parts_of[n][:, e, k : k + 1])

        def sums_stage(n):
            rows, tiles = summed_part(n)
            spread = psum_spread.tile([P, PACK], F32, tag="spread")
            sums_of[n] = spread[:, rows[0] : rows[-1] + 1]
            for t in rows:
                for group, j in tiles:
                    nc.tensor.matmul(
                        out=spread[:, t : t + 1], lhsT=features_of(group, t, j), rhs=ones[:], start=(group, j) == tiles[0], stop=(group, j) == tiles[-1]
                    )

        def stats_tile(n):
            if n not in stats_of:
                stats = per_bin.tile([P, HALVES, GROUPS * CHUNKS + 1, STATS], F32)
                stats_of[n] = stats
                first_slot_of[n] = [GROUPS * CHUNKS] * HALVES
            return stats_of[n]

        def summed_statistics_stage(n, between):
            rows, tiles = summed_part(n)
            samples = len(tiles) * P
            first = rows[0] // PAIR
            pairs = "p (u e) -> p u e"
            sums = sums_of[n].rearrange(pairs, e=PAIR)
            slots = stats_tile(n)[:, first:, GROUPS * CHUNKS, :].rearrange("p u (e s) -> p u e s", e=PAIR)
            nc.vector.tensor_scalar_mul(out=slots[:, :, :, 1], in0=sums, scalar1=1.0 / samples)
            if n != GRAM_BIN:
                squares = per_bin.tile([P, PAIR], F32)
                squares_of[n] = squares[:]
                nc.vector.reduce_sum(out=squares[:], in_=parts_of[n][:], axis=mybir.AxisListType.X)
            between[0]()
            sum_mean = per_bin.tile([P, HALVES, PAIR], F32)
            nc.vector.tensor_mul(out=sum_mean[:, first:, :], in0=sums, in1=slots[:, :, :, 1])
            between[1]()
            nc.vector.tensor_sub(out=slots[:, :, :, 2], in0=squares_of[n].rearrange(pairs, e=PAIR), in1=sum_mean[:, first:, :])
            nc.vector.memset(slots[:, :, :, 0], float(samples))

        def statistics_stage(group, u, between=()):
            n = group // GROUPS
            stats = stats_tile(n)
            values = turned_of[group][:, u * COLS : (u + 1) * COLS].bitcast(BF16)
            for h in range(CHUNKS):
                if is_scalar(group) and (u, h) == (HALVES - 1, CHUNKS - 1):
                    continue
                first_slot_of[n][u] -= 1
                nc.vector.bn_stats(out=stats[:, u, first_slot_of[n][u], :], in_=values[:, h * BN_CHUNK : (h + 1) * BN_CHUNK])
                if between:
                    between[h]()

        def moments_stage(n):
            moments = per_bin.tile([P, PACK, 2], F32)
            moments_of[n] = moments

            def row_moments(t):
                u, e = divmod(t, PAIR)
                last = GROUPS * CHUNKS + (t in summed_part(n)[0])
                nc.vector.bn_aggr(out=moments[:, t, :], in_=stats_of[n][:, u, first_slot_of[n][u] : last, 3 * e : 3 * e + 3])

            rows = list(range(PACK))
            if n != GRAM_BIN and scalar_groups(n):
                summed_statistics_stage(n, [lambda: row_moments(0), lambda: row_moments(1)])
                rows = rows[PAIR:]
            for t in rows:
                row_moments(t)

        def deviation_stage(n):
            rstd = per_bin.tile([P, PACK], F32)
            deviation_of[n] = rstd
            nc.scalar.activation(out=rstd[:], in_=moments_of[n][:, :, 1], func=ACT.Abs_reciprocal_sqrt, bias=BN_EPS)

        def coefficients_stage(n):
            gain = per_bin.tile([P, PACK], F32)
            gain_mean = per_bin.tile([P, PACK], F32)
            shift = per_bin.tile([P, PACK], F32)
            coefficients_of[n] = (gain, shift)
            return [
                lambda: nc.vector.tensor_mul(out=gain[:], in0=gb_t[:, n, :], in1=deviation_of[n][:]),
                lambda: nc.vector.tensor_mul(out=gain_mean[:], in0=gain[:], in1=moments_of[n][:, :, 0]),
                lambda: nc.vector.tensor_sub(out=shift[:], in0=gb_t[:, BINS + n, :], in1=gain_mean[:]),
            ]

        def gpsimd_rows_of(group):
            if group == 0:
                return R0
            if group < NEARLY:
                return RN
            return PACK if is_group(group + AFFINE_LAG - STATS_LAG) else SHARED_GPSIMD_ROWS

        def affine_stage(group):
            gain, shift = coefficients_of[group // GROUPS]
            gpsimd_rows = gpsimd_rows_of(group)
            whole = columns.tile([P, PACK * COLS * 3 // 2], F32, align_bytes=64)
            y_t = whole[:, 0 : PACK * COLS].rearrange("p (t c) -> p t c", t=PACK)
            columns_of[("samples", group)] = y_t
            grouped_of[("samples", group)] = whole[:, PACK * COLS :].bitcast(BF16).rearrange("p (c t) -> p c t", t=PACK)
            for u in range(HALVES):
                values = turned_of[group][:, u * COLS : (u + 1) * COLS].bitcast(BF16).rearrange("p (c e) -> p c e", e=PAIR)
                for e in range(PAIR):
                    t = PAIR * u + e
                    engine = nc.gpsimd if t < gpsimd_rows else nc.vector
                    engine.tensor_scalar(
                        out=y_t[:, t, :], in0=values[:, :, e], scalar1=gain[:, t : t + 1], scalar2=shift[:, t : t + 1], op0=ALU.mult, op1=ALU.add
                    )

        def turn_gamma_and_beta():
            spread = psum_spread.tile([P, COLS], F32, tag="spread")
            gb_bank[0] = spread
            for u in range(HALVES):
                nc.tensor.transpose(out=spread[:, u * P : (u + 1) * P], in_=gb_rows[:, u * P : (u + 1) * P], identity=ident[:])

        def keep_gamma_and_beta():
            nc.vector.tensor_copy(
                out=gb_t[:].rearrange("p r (u e) -> p r u e", e=PAIR),
                in_=gb_bank[0][:, 0 : HALVES * P].bitcast(BF16).rearrange("p (u r e) -> p r u e", u=HALVES, e=PAIR)[:, 0 : 2 * BINS, :, :],
            )


        def squares_stage(key, tiles):
            x_t = columns_of[key]
            samples = key[0] == "samples"
            if key not in norm_sq_of:
                norm_sq = small.tile([P, GROUP], F32)
                norm_sq_of[key] = norm_sq
            for j in tiles:
                if samples:
                    back = psum_scalar.tile([P, PACK * P], F32, tag="bank")
                else:
                    back = psum_spread.tile([P, PACK * P], BF16, tag="spread")
                for t in range(PACK):
                    nc.tensor.transpose(
                        out=back[:, t * P : (t + 1) * P], in_=x_t[:, t, j * P : (j + 1) * P], identity=ident[:] if samples else ident_bf[:]
                    )
                squares = scrap.tile([P, PACK * P], BF16)
                nc.scalar.activation(out=squares[:], in_=back[:], func=ACT.Square, accum_out=norm_sq_of[key][:, j : j + 1])

        def inverse_stage(key):
            tiles = tiles_of(key)
            inverse = small.tile([P, GROUP], F32)
            inverse_of[key] = inverse
            nc.scalar.activation(out=inverse[:, 0:tiles], in_=norm_sq_of[key][:, 0:tiles], func=ACT.Abs_reciprocal_sqrt, bias=L2_EPS * L2_EPS)

        def spread_stage(key):
            spread = psum_spread.tile([P, COLS], F32, tag="spread")
            spread_of[key] = spread
            for j in range(tiles_of(key)):
                nc.tensor.transpose(out=spread[:, j * P : (j + 1) * P], in_=inverse_of[key][:, j : j + 1].to_broadcast([P, P]), identity=ident[:])

        def columns_of_half(key, half):
            cols = tiles_of(key) * P
            return slice(0, cols) if half is None else slice(half * cols // 2, (half + 1) * cols // 2)

        def scale_stage(key, half=None):
            cols = columns_of_half(key, half)
            count = cols.stop - cols.start
            if key not in grouped_of:
                grouped = quant.tile([P, CLASSES, PACK], BF16, align_bytes=64)
                grouped_of[key] = grouped[:]
            nc.vector.tensor_tensor(
                out=grouped_of[key][:, cols, :].rearrange("p (c i) t -> p c t i", i=RUN),
                in0=columns_of[key][:, :, cols].rearrange("p t (c i) -> p c t i", i=RUN),
                in1=spread_of[key][:, cols].rearrange("p (c i) -> p c i", i=RUN).unsqueeze(2).to_broadcast([P, count // RUN, PACK, RUN]),
                op=ALU.mult,
            )

        def quantise_stage(key, half=None):
            cols = columns_of_half(key, half)
            if key not in operand_of:
                if key[0] == "samples":
                    codes = quant.tile([P, COLS], U32, align_bytes=64)
                    plane = quant.tile([P, COLS], U8, align_bytes=64)
                    operand_of[key] = (codes[:], plane[:])
                else:
                    operand_of[key] = (fc_codes[:, key[1], :], fc_planes[:, key[1], :])
            codes, plane = operand_of[key]
            nc.vector.quantize_mx(
                out=codes[:, cols].bitcast(FP8X4), scales=plane[:, cols], in_=grouped_of[key][:, cols, :].rearrange("p c t -> p (c t)")
            )


        def matmul_stage(group, half):
            codes, plane = operand_of[("samples", group)]
            class_codes, class_plane = operand_of[("classes", group // GROUPS)]
            acc = psum_scalar.tile([P, BANK_TILES, CLASSES], F32, tag="bank")
            product_of[group, half] = acc
            for i in range(BANK_TILES):
                samples = slice((half * BANK_TILES + i) * P, (half * BANK_TILES + i + 1) * P)
                nc.tensor.matmul_mx(
                    out=acc[:, i, :],
                    lhsT=codes[:, samples].bitcast(FP8X4),
                    lhsT_scale=plane[:, samples],
                    rhs=class_codes.bitcast(FP8X4),
                    rhs_scale=class_plane,
                    start=True,
                    stop=True,
                )

        def leave_stage(group, half):
            if half == 0:
                logits = results.tile([P, GROUP, CLASSES], F32)
                logits_of[group] = logits
            nc.scalar.copy(out=logits_of[group][:, half * BANK_TILES : (half + 1) * BANK_TILES, :], in_=product_of[group, half][:])

        def store_stage(group, tiles):
            n, g = divmod(group, GROUPS)
            nc.sync.dma_start(out=out_tiles[:, g * GROUP + tiles.start : g * GROUP + tiles.stop, n, :], in_=logits_of[group][:, tiles, :])

        order = LOAD_ORDER
        for group in order:
            load_stage(group)
            if group == FC_AFTER:
                nc.sync.dma_start(out=fc_raw[:], in_=fc1d.rearrange("n (u p e) k -> p (n u) (e k)", u=HALVES, e=PAIR))
        for step in range(LAST_STEP + 1):
            if is_group(step + LOAD_LEAD) and step + LOAD_LEAD not in order:
                load_stage(step + LOAD_LEAD)

            for n in bin_due(step, COEFFICIENTS_LAG):
                deviation_stage(n)

            for key in columns_due(step - QUANTISE_AFTER) + classes_scaled(step - 1):
                if key not in operand_of:
                    quantise_stage(key)
            if step == SMALL_INPUTS_STEP + 1:
                keep_gamma_and_beta()
            bn_group = is_group(step - STATS_LAG) and not is_gram(step - STATS_LAG)
            coefficients = [part for n in bin_due(step, COEFFICIENTS_LAG) for part in coefficients_stage(n)]
            if coefficients:
                coefficients[0]()
            if bn_group:
                statistics_stage(step - STATS_LAG, 0, coefficients[1:])
            elif coefficients:
                coefficients[1]()
                coefficients[2]()
            if step == COEFFICIENTS_LAG:
                affine_stage(0)

            turn, square, product = step, step - SQUARES_LAG, step - SQUARES_LAG - MATMUL_AFTER
            if is_group(square):
                squares_stage(("samples", square), range(0, GROUP // 2))
            for key in columns_due(step - SCALE_AFTER) + classes_scaled(step):
                spread_stage(key)
            if is_group(square):
                squares_stage(("samples", square), range(GROUP // 2, GROUP))
            if is_group(product) and product != LAST_GROUP:
                matmul_stage(product, 0)
                matmul_stage(product, 1)
                leave_stage(product, 0)
            if is_group(square):
                inverse_stage(("samples", square))
            if is_group(product) and product != LAST_GROUP:
                leave_stage(product, 1)
                store_stage(product, slice(0, GROUP))
            if is_group(step - STATS_LAG) and is_scalar(step - STATS_LAG):
                scalar_squares_stage(step - STATS_LAG)
            if is_group(turn):
                turn_stage(turn)
            if is_group(turn + GRAM_LEAD) and is_gram(turn + GRAM_LEAD):
                gram_stage(turn + GRAM_LEAD)
            for n in bin_due(step, GROUPS - 1):
                if n != GRAM_BIN and scalar_groups(n):
                    sums_stage(n)
            if step == GRAM_END:
                sums_stage(GRAM_BIN)
            if step == SMALL_INPUTS_STEP:
                turn_gamma_and_beta()
            for key in classes_due(step):
                squares_stage(key, range(CLASS_TILES))
                inverse_stage(key)

            if is_group(step - AFFINE_LAG) and step > AFFINE_LAG:
                affine_stage(step - AFFINE_LAG)
            for key in columns_due(step - SCALE_AFTER) + classes_scaled(step):
                if key == ("samples", LAST_GROUP):
                    for half in range(GROUP // BANK_TILES):
                        scale_stage(key, half)
                        quantise_stage(key, half)
                        matmul_stage(LAST_GROUP, half)
                        leave_stage(LAST_GROUP, half)
                        store_stage(LAST_GROUP, slice(half * BANK_TILES, (half + 1) * BANK_TILES))
                else:
                    scale_stage(key)
            if bn_group:
                statistics_stage(step - STATS_LAG, 1)
            if step == GRAM_END + 1:
                summed_statistics_stage(GRAM_BIN, [gram_squares_stage, lambda: None])
            for n in bin_due(step, MOMENTS_LAG):
                moments_stage(n)
